import numpy as np
import ml_dtypes


def mxq(x, axis, fmt="e4m3"):
    dtype, down = {"e4m3": (ml_dtypes.float8_e4m3fn, 7), "e5m2": (ml_dtypes.float8_e5m2, 14)}[fmt]
    v = np.moveaxis(np.asarray(x, np.float32).astype(ml_dtypes.bfloat16).astype(np.float64), axis, -1)
    blocks = v.reshape(v.shape[:-1] + (-1, 32))
    amax = np.abs(blocks).max(-1, keepdims=True)
    byte = np.maximum(np.where(amax > 0, np.frexp(amax)[1] - 1 + 127, 0) - down, 1)
    scale = np.exp2(byte - 127.0)
    codes = (blocks / scale).astype(np.float32).astype(dtype).astype(np.float64)
    return np.moveaxis((codes * scale).reshape(v.shape), -1, axis)


WIDE = False


def mx_kscale(k):
    if not WIDE:
        return np.ones(k)
    levels = np.array([10, -10, 5, -5, 0])
    a = np.random.permutation(np.resize(levels, k // 512 * 4)).reshape(k // 512, 4)
    idx = np.arange(k)
    return np.exp2(a[idx // 512, idx % 128 // 32])


BF16 = ml_dtypes.bfloat16


def bf(x):
    return np.asarray(x, np.float32).astype(BF16)


def f64(x):
    return np.asarray(x).astype(np.float64)


B, C, H, D, N, CO = 4, 4096, 2048, 128, 4, 512
NC = N * C
EPS = 1e-5


def bn(v, gamma, beta, axes):
    mean = v.mean(axis=axes, keepdims=True)
    var = v.var(axis=axes, keepdims=True)
    return (v - mean) / np.sqrt(var + EPS) * gamma + beta


def setup_inputs():
    u = mx_kscale(NC)
    head = np.maximum(np.random.standard_normal((N, B, C, D)), 0.0) + 0.25 * np.random.standard_normal((N, B, C, D))
    return {'head_res': bf(head * u.reshape(N, 1, C, 1)),
            'W_merge': bf(np.random.standard_normal((CO, NC)) / np.sqrt(NC) / u[None, :]),
            'g_m': bf(1.0 + 0.1 * np.random.standard_normal(CO)),
            'b_m': bf(0.1 * np.random.standard_normal(CO))}


def reference(head_res, W_merge, g_m, b_m):
    cat = f64(head_res).transpose(1, 0, 2, 3).reshape(B, NC, D)
    m = mxq(f64(W_merge), 1, 'e4m3')[None] @ mxq(cat, 1, 'e4m3')
    m = bn(m, f64(g_m)[None, :, None], f64(b_m)[None, :, None], (0, 2))
    return np.maximum(m, 0.0)

@@ -1,0 +1,221 @@
+from contextlib import ExitStack
+
+import concourse.mybir as mybir
+from concourse.masks import make_identity
+
+F32 = mybir.dt.float32
+BF16 = mybir.dt.bfloat16
+U32 = mybir.dt.uint32
+U8 = mybir.dt.uint8
+FP8X4 = mybir.dt.float8_e4m3fn_x4
+ACT = mybir.ActivationFunctionType
+
+P = 128
+PACK = 4
+K_PASS = P * PACK
+PAIR = 2
+
+HEADS, SAMPLES, CHANNELS, POSITIONS = 4, 4, 4096, 128
+OUT_CHANNELS = 512
+EPS = 1e-5
+
+O_TILES = OUT_CHANNELS // P
+COLUMNS = SAMPLES * POSITIONS
+HEAD_PASSES = CHANNELS // K_PASS
+PASSES = HEADS * HEAD_PASSES
+SLABS = HEADS * O_TILES
+BANK_PASSES = 2
+HALF_PASSES = HEAD_PASSES // 2
+HALF_WORDS = HALF_PASSES * P
+STEP_PASSES = 2
+LEAD = O_TILES
+STEPS = SLABS + LEAD
+AHEAD = 4
+RUN = 4
+
+FLOPS = 2 * OUT_CHANNELS * HEADS * CHANNELS * COLUMNS
+
+
+def tile_block_height_reducing_filtering_pb_k_kernel(tc, head_res, W_merge, g_m, b_m, out):
+    nc = tc.nc
+    with ExitStack() as ctx:
+        const = ctx.enter_context(tc.tile_pool(name="const", bufs=1))
+        w_raw_pool = ctx.enter_context(tc.tile_pool(name="w_raw", bufs=AHEAD + 1))
+        c_raw_pool = ctx.enter_context(tc.tile_pool(name="c_raw", bufs=STEP_PASSES * (AHEAD + 1)))
+        w_grouped_pool = ctx.enter_context(tc.tile_pool(name="w_grouped", bufs=3))
+        c_grouped_pool = ctx.enter_context(tc.tile_pool(name="c_grouped", bufs=3))
+        w_mx_pool = ctx.enter_context(tc.tile_pool(name="w_mx", bufs=SLABS))
+        c_mx_pool = ctx.enter_context(tc.tile_pool(name="c_mx", bufs=4))
+        result_pool = ctx.enter_context(tc.tile_pool(name="result", bufs=O_TILES))
+        acc_pool = ctx.enter_context(tc.psum_pool(name="acc", bufs=O_TILES))
+        wt_pool = ctx.enter_context(tc.psum_pool(name="wt", bufs=4))
+        ctx.enter_context(tc.manual_schedule())
+
+        w_raws, w_groupeds, w_codes, w_scales = {}, {}, {}, {}
+        c_raws, c_groupeds, c_codes, c_scales = {}, {}, {}, {}
+
+        ident = const.tile([P, P], F32)
+        make_identity(nc, ident[:])
+        eps = const.tile([P, 1], F32)
+        nc.vector.memset(eps[:], EPS)
+        first_sqrt = const.tile([P, 1], F32)
+        nc.scalar.activation(out=first_sqrt[:], in_=eps[:], func=ACT.Sqrt)
+
+        gb_rows = const.tile([P, P], BF16)
+        nc.vector.memset(gb_rows[:], 0.0)
+        nc.scalar.dma_start(out=gb_rows[0:O_TILES, :], in_=g_m.rearrange("(t o) -> t o", o=P))
+        nc.scalar.dma_start(out=gb_rows[O_TILES : 2 * O_TILES, :], in_=b_m.rearrange("(t o) -> t o", o=P))
+        gb_rows_f32 = const.tile([P, P], F32)
+        nc.vector.tensor_copy(out=gb_rows_f32[:], in_=gb_rows[:])
+        gb_bank = wt_pool.tile([P, P], F32, tag="wt")
+        nc.tensor.transpose(gb_bank[:], gb_rows_f32[:], ident[:])
+        gb = const.tile([P, 2 * O_TILES], F32)
+        nc.vector.tensor_copy(out=gb[:], in_=gb_bank[:, 0 : 2 * O_TILES])
+
+        acc = []
+        for t in range(O_TILES):
+            acc_t = acc_pool.tile([P, COLUMNS], F32, tag="acc")
+            acc.append(acc_t)
+
+        def load_slab(u):
+            if not 0 <= u < SLABS:
+                return
+            n, t = divmod(u, O_TILES)
+            w_raw = w_raw_pool.tile([P, CHANNELS], BF16)
+            nc.sync.dma_start(
+                out=w_raw[:], in_=W_merge[t * P : (t + 1) * P, n * CHANNELS : (n + 1) * CHANNELS]
+            )
+            w_raws[u] = w_raw
+
+        def load_pass(q):
+            if not 0 <= q < PASSES:
+                return
+            n, g = divmod(q, HEAD_PASSES)
+            c_raw = c_raw_pool.tile([P, SAMPLES, PACK * POSITIONS], BF16)
+            rows = head_res[n, :, g * K_PASS : (g + 1) * K_PASS, :]
+            nc.sync.dma_start(out=c_raw[:], in_=rows.rearrange("b (p j) w -> p b (j w)", j=PACK))
+            c_raws[q] = c_raw
+
+        def transpose_half_slab(u, half):
+            if not 0 <= u < SLABS:
+                return
+            if half == 0:
+                w_grouped = w_grouped_pool.tile([P, HEAD_PASSES, P, PACK], BF16, align_bytes=64)
+                w_groupeds[u] = w_grouped
+            words = w_raws[u][:].bitcast(F32).rearrange("o (g p s) -> o g s p", p=P, s=PAIR)
+            grouped_words = w_groupeds[u][:].bitcast(F32)
+            first = half * HALF_PASSES
+            for g0 in range(first, first + HALF_PASSES, BANK_PASSES):
+                wt = wt_pool.tile([P, BANK_PASSES, PAIR, P], F32)
+                for i in range(BANK_PASSES):
+                    for s in range(PAIR):
+                        nc.tensor.transpose(wt[:, i, s, :], words[:, g0 + i, s, :], ident[:])
+                nc.scalar.copy(
+                    out=grouped_words[:, g0 : g0 + BANK_PASSES, :, :],
+                    in_=wt[:].rearrange("p g s o -> p g o s"),
+                )
+
+        def quantise_half_slab(u, half):
+            if not 0 <= u < SLABS:
+                return
+            if half == 0:
+                w_code = w_mx_pool.tile([P, HEAD_PASSES * P], U32, align_bytes=64)
+                w_scale = w_mx_pool.tile([P, HEAD_PASSES * P], U8, align_bytes=64)
+                w_codes[u], w_scales[u] = w_code, w_scale
+            passes = slice(half * HALF_PASSES, (half + 1) * HALF_PASSES)
+            cols = slice(half * HALF_WORDS, (half + 1) * HALF_WORDS)
+            nc.vector.quantize_mx(
+                out=w_codes[u][:, cols].bitcast(FP8X4),
+                scales=w_scales[u][:, cols],
+                in_=w_groupeds[u][:, passes, :, :].rearrange("p g o t -> p (g o t)"),
+            )
+
+        def regroup_pass(q):
+            if not 0 <= q < PASSES:
+                return
+            c_grouped = c_grouped_pool.tile([P, COLUMNS, PACK], BF16, align_bytes=64)
+            c_groupeds[q] = c_grouped
+            src = c_raws[q][:].rearrange("p b (t c i) -> p b c t i", t=PACK, i=RUN)
+            dst = c_grouped[:].rearrange("p (b c i) t -> p b c t i", b=SAMPLES, i=RUN)
+            scalar_samples = 1 if q // STEP_PASSES + LEAD < SLABS else 2
+            vector_samples = SAMPLES - scalar_samples
+            nc.vector.tensor_copy(out=dst[:, 0:vector_samples], in_=src[:, 0:vector_samples])
+            for b in range(vector_samples, SAMPLES):
+                nc.scalar.copy(out=dst[:, b], in_=src[:, b])
+
+        def quantise_pass(q):
+            if not 0 <= q < PASSES:
+                return
+            c_code = c_mx_pool.tile([P, COLUMNS], U32, align_bytes=64)
+            c_scale = c_mx_pool.tile([P, COLUMNS], U8, align_bytes=64)
+            c_codes[q], c_scales[q] = c_code, c_scale
+            nc.vector.quantize_mx(
+                out=c_code[:].bitcast(FP8X4),
+                scales=c_scale[:],
+                in_=c_groupeds[q][:].rearrange("p c t -> p (c t)"),
+            )
+
+        def multiply_pass(q):
+            if not 0 <= q < PASSES:
+                return
+            n, g = divmod(q, HEAD_PASSES)
+            cols = slice(g * P, (g + 1) * P)
+            for t in range(O_TILES):
+                u = n * O_TILES + t
+                nc.tensor.matmul_mx(
+                    out=acc[t][:],
+                    lhsT=w_codes[u][:, cols].bitcast(FP8X4),
+                    lhsT_scale=w_scales[u][:, cols],
+                    rhs=c_codes[q][:].bitcast(FP8X4),
+                    rhs_scale=c_scales[q][:],
+                    start=(q == 0),
+                    stop=(q == PASSES - 1),
+                )
+
+        def load_step(s):
+            load_slab(s)
+            load_pass(STEP_PASSES * (s - LEAD))
+            load_pass(STEP_PASSES * (s - LEAD) + 1)
+
+        for s in range(AHEAD):
+            load_step(s)
+        for s in range(STEPS):
+            q = STEP_PASSES * (s - LEAD)
+            load_step(s + AHEAD)
+            transpose_half_slab(s, 0)
+            regroup_pass(q)
+            transpose_half_slab(s, 1)
+            multiply_pass(q - 1)
+            quantise_half_slab(s - 1, 0)
+            quantise_pass(q)
+            multiply_pass(q)
+            regroup_pass(q + 1)
+            quantise_half_slab(s - 1, 1)
+            quantise_pass(q + 1)
+        multiply_pass(PASSES - 1)
+
+        stats = const.tile([P, O_TILES, 6], F32)
+        mean_var = const.tile([P, O_TILES, 2], F32)
+        for t in range(O_TILES):
+            nc.vector.bn_stats(out=stats[:, t, :], in_=acc[t][:])
+            nc.vector.bn_aggr(out=mean_var[:, t, :], in_=stats[:, t, :])
+        mean, var = mean_var[:, :, 0], mean_var[:, :, 1]
+        std = const.tile([P, O_TILES], F32)
+        nc.scalar.activation(out=std[:], in_=var, func=ACT.Sqrt, bias=eps[:, 0:1], scale=1.0)
+        inv_std = const.tile([P, O_TILES], F32)
+        nc.vector.reciprocal(out=inv_std[:], in_=std[:])
+        gain = const.tile([P, O_TILES], F32)
+        nc.vector.tensor_mul(out=gain[:], in0=gb[:, 0:O_TILES], in1=inv_std[:])
+        mean_gain = const.tile([P, O_TILES], F32)
+        nc.vector.tensor_mul(out=mean_gain[:], in0=mean, in1=gain[:])
+        shift = const.tile([P, O_TILES], F32)
+        nc.vector.tensor_sub(out=shift[:], in0=gb[:, O_TILES : 2 * O_TILES], in1=mean_gain[:])
+        for t in range(O_TILES):
+            result = result_pool.tile([P, COLUMNS], F32)
+            nc.scalar.activation(
+                out=result[:], in_=acc[t][:], func=ACT.Relu, bias=shift[:, t : t + 1], scale=gain[:, t : t + 1]
+            )
+            nc.sync.dma_start(
+                out=out[:, t * P : (t + 1) * P, :].rearrange("b o d -> o b d"),
+                in_=result[:].rearrange("o (b d) -> o b d", b=SAMPLES),
+            )

@@ -54,23 +54,18 @@ def tile_block_height_reducing_filtering_pb_k_kernel(tc, head_res, W_merge, g_m,
         w_raws, w_groupeds, w_codes, w_scales = {}, {}, {}, {}
         c_raws, c_groupeds, c_codes, c_scales = {}, {}, {}, {}
 
-        ident = const.tile([P, P], F32)
-        make_identity(nc, ident[:])
-        eps = const.tile([P, 1], F32)
-        nc.vector.memset(eps[:], EPS)
-        first_sqrt = const.tile([P, 1], F32)
-        nc.scalar.activation(out=first_sqrt[:], in_=eps[:], func=ACT.Sqrt)
-
         gb_rows = const.tile([P, P], BF16)
         nc.vector.memset(gb_rows[:], 0.0)
         nc.scalar.dma_start(out=gb_rows[0:O_TILES, :], in_=g_m.rearrange("(t o) -> t o", o=P))
         nc.scalar.dma_start(out=gb_rows[O_TILES : 2 * O_TILES, :], in_=b_m.rearrange("(t o) -> t o", o=P))
-        gb_rows_f32 = const.tile([P, P], F32)
-        nc.vector.tensor_copy(out=gb_rows_f32[:], in_=gb_rows[:])
-        gb_bank = wt_pool.tile([P, P], F32, tag="wt")
-        nc.tensor.transpose(gb_bank[:], gb_rows_f32[:], ident[:])
-        gb = const.tile([P, 2 * O_TILES], F32)
-        nc.vector.tensor_copy(out=gb[:], in_=gb_bank[:, 0 : 2 * O_TILES])
+        ident = const.tile([P, P], F32)
+        make_identity(nc, ident[:])
+        ident_bf16 = const.tile([P, P], BF16)
+        make_identity(nc, ident_bf16[:])
+        eps = const.tile([P, 1], F32)
+        nc.vector.memset(eps[:], EPS)
+        first_sqrt = const.tile([P, 1], F32)
+        nc.scalar.activation(out=first_sqrt[:], in_=eps[:], func=ACT.Sqrt)
 
         acc = []
         for t in range(O_TILES):
@@ -135,13 +130,13 @@ def tile_block_height_reducing_filtering_pb_k_kernel(tc, head_res, W_merge, g_m,
                 return
             c_grouped = c_grouped_pool.tile([P, COLUMNS, PACK], BF16, align_bytes=64)
             c_groupeds[q] = c_grouped
-            src = c_raws[q][:].rearrange("p b (t c i) -> p b c t i", t=PACK, i=RUN)
-            dst = c_grouped[:].rearrange("p (b c i) t -> p b c t i", b=SAMPLES, i=RUN)
+            src = c_raws[q][:].rearrange("p b (t c i) -> p c b t i", t=PACK, i=RUN)
+            dst = c_grouped[:].rearrange("p (b c i) t -> p c b t i", b=SAMPLES, i=RUN)
             scalar_samples = 1 if q // STEP_PASSES + LEAD < SLABS else 2
             vector_samples = SAMPLES - scalar_samples
-            nc.vector.tensor_copy(out=dst[:, 0:vector_samples], in_=src[:, 0:vector_samples])
+            nc.vector.tensor_copy(out=dst[:, :, 0:vector_samples], in_=src[:, :, 0:vector_samples])
             for b in range(vector_samples, SAMPLES):
-                nc.scalar.copy(out=dst[:, b], in_=src[:, b])
+                nc.scalar.copy(out=dst[:, :, b], in_=src[:, :, b])
 
         def quantise_pass(q):
             if not 0 <= q < PASSES:
@@ -192,6 +187,10 @@ def tile_block_height_reducing_filtering_pb_k_kernel(tc, head_res, W_merge, g_m,
             regroup_pass(q + 1)
             quantise_half_slab(s - 1, 1)
             quantise_pass(q + 1)
+        gb_bank = wt_pool.tile([P, P], BF16, tag="wt")
+        nc.tensor.transpose(gb_bank[:], gb_rows[:], ident_bf16[:])
+        gb = const.tile([P, 2 * O_TILES], F32)
+        nc.scalar.copy(out=gb[:], in_=gb_bank[:, 0 : 2 * O_TILES])
         multiply_pass(PASSES - 1)
 
         stats = const.tile([P, O_TILES, 6], F32)

@@ -87,8 +87,14 @@ def tile_block_height_reducing_filtering_pb_k_kernel(tc, head_res, W_merge, g_m,
                 return
             n, g = divmod(q, HEAD_PASSES)
             c_raw = c_raw_pool.tile([P, SAMPLES, PACK * POSITIONS], BF16)
-            rows = head_res[n, :, g * K_PASS : (g + 1) * K_PASS, :]
-            nc.sync.dma_start(out=c_raw[:], in_=rows.rearrange("b (p j) w -> p b (j w)", j=PACK))
+            half_width = PAIR * POSITIONS
+            for s in range(PAIR):
+                first = g * K_PASS + s * PAIR * P
+                rows = head_res[n, :, first : first + PAIR * P, :]
+                nc.sync.dma_start(
+                    out=c_raw[:, :, s * half_width : (s + 1) * half_width],
+                    in_=rows.rearrange("b (p e) w -> p b (e w)", e=PAIR),
+                )
             c_raws[q] = c_raw
 
         def transpose_half_slab(u, half):
@@ -97,7 +103,7 @@ def tile_block_height_reducing_filtering_pb_k_kernel(tc, head_res, W_merge, g_m,
             if half == 0:
                 w_grouped = w_grouped_pool.tile([P, HEAD_PASSES, P, PACK], BF16, align_bytes=64)
                 w_groupeds[u] = w_grouped
-            words = w_raws[u][:].bitcast(F32).rearrange("o (g p s) -> o g s p", p=P, s=PAIR)
+            words = w_raws[u][:].bitcast(F32).rearrange("o (g s p) -> o g s p", p=P, s=PAIR)
             grouped_words = w_groupeds[u][:].bitcast(F32)
             first = half * HALF_PASSES
             for g0 in range(first, first + HALF_PASSES, BANK_PASSES):

@@ -9,6 +9,7 @@ U32 = mybir.dt.uint32
 U8 = mybir.dt.uint8
 FP8X4 = mybir.dt.float8_e4m3fn_x4
 ACT = mybir.ActivationFunctionType
+ALU = mybir.AluOpType
 
 P = 128
 PACK = 4
@@ -30,6 +31,7 @@ HALF_WORDS = HALF_PASSES * P
 STEP_PASSES = 2
 LEAD = O_TILES
 STEPS = SLABS + LEAD
+DRAIN = 2
 AHEAD = 4
 RUN = 4
 
@@ -43,9 +45,9 @@ def tile_block_height_reducing_filtering_pb_k_kernel(tc, head_res, W_merge, g_m,
         w_raw_pool = ctx.enter_context(tc.tile_pool(name="w_raw", bufs=AHEAD + 1))
         c_raw_pool = ctx.enter_context(tc.tile_pool(name="c_raw", bufs=STEP_PASSES * (AHEAD + 1)))
         w_grouped_pool = ctx.enter_context(tc.tile_pool(name="w_grouped", bufs=3))
-        c_grouped_pool = ctx.enter_context(tc.tile_pool(name="c_grouped", bufs=3))
+        c_grouped_pool = ctx.enter_context(tc.tile_pool(name="c_grouped", bufs=4))
         w_mx_pool = ctx.enter_context(tc.tile_pool(name="w_mx", bufs=SLABS))
-        c_mx_pool = ctx.enter_context(tc.tile_pool(name="c_mx", bufs=4))
+        c_mx_pool = ctx.enter_context(tc.tile_pool(name="c_mx", bufs=6))
         result_pool = ctx.enter_context(tc.tile_pool(name="result", bufs=O_TILES))
         acc_pool = ctx.enter_context(tc.psum_pool(name="acc", bufs=O_TILES))
         wt_pool = ctx.enter_context(tc.psum_pool(name="wt", bufs=4))
@@ -87,14 +89,8 @@ def tile_block_height_reducing_filtering_pb_k_kernel(tc, head_res, W_merge, g_m,
                 return
             n, g = divmod(q, HEAD_PASSES)
             c_raw = c_raw_pool.tile([P, SAMPLES, PACK * POSITIONS], BF16)
-            half_width = PAIR * POSITIONS
-            for s in range(PAIR):
-                first = g * K_PASS + s * PAIR * P
-                rows = head_res[n, :, first : first + PAIR * P, :]
-                nc.sync.dma_start(
-                    out=c_raw[:, :, s * half_width : (s + 1) * half_width],
-                    in_=rows.rearrange("b (p e) w -> p b (e w)", e=PAIR),
-                )
+            rows = head_res[n, :, g * K_PASS : (g + 1) * K_PASS, :]
+            nc.sync.dma_start(out=c_raw[:], in_=rows.rearrange("b (p j) w -> p b (j w)", j=PACK))
             c_raws[q] = c_raw
 
         def transpose_half_slab(u, half):
@@ -103,7 +99,7 @@ def tile_block_height_reducing_filtering_pb_k_kernel(tc, head_res, W_merge, g_m,
             if half == 0:
                 w_grouped = w_grouped_pool.tile([P, HEAD_PASSES, P, PACK], BF16, align_bytes=64)
                 w_groupeds[u] = w_grouped
-            words = w_raws[u][:].bitcast(F32).rearrange("o (g s p) -> o g s p", p=P, s=PAIR)
+            words = w_raws[u][:].bitcast(F32).rearrange("o (g p s) -> o g s p", p=P, s=PAIR)
             grouped_words = w_groupeds[u][:].bitcast(F32)
             first = half * HALF_PASSES
             for g0 in range(first, first + HALF_PASSES, BANK_PASSES):
@@ -180,24 +176,25 @@ def tile_block_height_reducing_filtering_pb_k_kernel(tc, head_res, W_merge, g_m,
 
         for s in range(AHEAD):
             load_step(s)
-        for s in range(STEPS):
+        for s in range(STEPS + DRAIN):
             q = STEP_PASSES * (s - LEAD)
             load_step(s + AHEAD)
             transpose_half_slab(s, 0)
             regroup_pass(q)
             transpose_half_slab(s, 1)
-            multiply_pass(q - 1)
+            multiply_pass(q - 3)
+            multiply_pass(q - 2)
             quantise_half_slab(s - 1, 0)
-            quantise_pass(q)
-            multiply_pass(q)
+            quantise_pass(q - 1)
             regroup_pass(q + 1)
             quantise_half_slab(s - 1, 1)
-            quantise_pass(q + 1)
+            quantise_pass(q)
+
         gb_bank = wt_pool.tile([P, P], BF16, tag="wt")
         nc.tensor.transpose(gb_bank[:], gb_rows[:], ident_bf16[:])
         gb = const.tile([P, 2 * O_TILES], F32)
         nc.scalar.copy(out=gb[:], in_=gb_bank[:, 0 : 2 * O_TILES])
-        multiply_pass(PASSES - 1)
+        g_cols, b_cols = gb[:, 0:O_TILES], gb[:, O_TILES : 2 * O_TILES]
 
         stats = const.tile([P, O_TILES, 6], F32)
         mean_var = const.tile([P, O_TILES, 2], F32)
@@ -207,20 +204,42 @@ def tile_block_height_reducing_filtering_pb_k_kernel(tc, head_res, W_merge, g_m,
         mean, var = mean_var[:, :, 0], mean_var[:, :, 1]
         std = const.tile([P, O_TILES], F32)
         nc.scalar.activation(out=std[:], in_=var, func=ACT.Sqrt, bias=eps[:, 0:1], scale=1.0)
+        mean_g = const.tile([P, O_TILES], F32)
+        nc.vector.tensor_mul(out=mean_g[:], in0=mean, in1=g_cols)
         inv_std = const.tile([P, O_TILES], F32)
         nc.vector.reciprocal(out=inv_std[:], in_=std[:])
         gain = const.tile([P, O_TILES], F32)
-        nc.vector.tensor_mul(out=gain[:], in0=gb[:, 0:O_TILES], in1=inv_std[:])
+        nc.vector.tensor_mul(out=gain[:], in0=g_cols, in1=inv_std[:])
         mean_gain = const.tile([P, O_TILES], F32)
-        nc.vector.tensor_mul(out=mean_gain[:], in0=mean, in1=gain[:])
+        nc.vector.tensor_mul(out=mean_gain[:], in0=mean_g[:], in1=inv_std[:])
         shift = const.tile([P, O_TILES], F32)
-        nc.vector.tensor_sub(out=shift[:], in0=gb[:, O_TILES : 2 * O_TILES], in1=mean_gain[:])
+        nc.vector.tensor_sub(out=shift[:], in0=b_cols, in1=mean_gain[:])
+
+        results = []
         for t in range(O_TILES):
             result = result_pool.tile([P, COLUMNS], F32)
-            nc.scalar.activation(
-                out=result[:], in_=acc[t][:], func=ACT.Relu, bias=shift[:, t : t + 1], scale=gain[:, t : t + 1]
-            )
+            results.append(result)
+
+        def store(t):
             nc.sync.dma_start(
                 out=out[:, t * P : (t + 1) * P, :].rearrange("b o d -> o b d"),
-                in_=result[:].rearrange("o (b d) -> o b d", b=SAMPLES),
+                in_=results[t][:].rearrange("o (b d) -> o b d", b=SAMPLES),
             )
+
+        for t in range(0, O_TILES, 2):
+            nc.scalar.activation(
+                out=results[t][:], in_=acc[t][:], func=ACT.Relu, bias=shift[:, t : t + 1], scale=gain[:, t : t + 1]
+            )
+            store(t)
+        for t in range(1, O_TILES, 2):
+            nc.vector.tensor_scalar(
+                out=results[t][:],
+                in0=acc[t][:],
+                scalar1=gain[:, t : t + 1],
+                scalar2=shift[:, t : t + 1],
+                op0=ALU.mult,
+                op1=ALU.add,
+            )
+        for t in range(1, O_TILES, 2):
+            nc.vector.tensor_scalar_max(out=results[t][:], in0=results[t][:], scalar1=0.0)
+            store(t)

@@ -22,18 +22,18 @@ EPS = 1e-5
 
 O_TILES = OUT_CHANNELS // P
 COLUMNS = SAMPLES * POSITIONS
-HEAD_PASSES = CHANNELS // K_PASS
-PASSES = HEADS * HEAD_PASSES
-SLABS = HEADS * O_TILES
+PASSES = HEADS * CHANNELS // K_PASS
+BLOCK_PASSES = 4
 BANK_PASSES = 2
-HALF_PASSES = HEAD_PASSES // 2
-HALF_WORDS = HALF_PASSES * P
+BLOCK_BANKS = BLOCK_PASSES // BANK_PASSES
+BANK_WORDS = BANK_PASSES * P
+CHUNKS = PASSES // BLOCK_PASSES
+STEP_BLOCKS = 2
 STEP_PASSES = 2
-LEAD = O_TILES
-STEPS = SLABS + LEAD
-DRAIN = 2
-AHEAD = 4
+STEPS = CHUNKS * O_TILES // STEP_BLOCKS
+AHEAD = 6
 RUN = 4
+GROUPS = POSITIONS // RUN
 
 FLOPS = 2 * OUT_CHANNELS * HEADS * CHANNELS * COLUMNS
 
@@ -42,11 +42,11 @@ def tile_block_height_reducing_filtering_pb_k_kernel(tc, head_res, W_merge, g_m,
     nc = tc.nc
     with ExitStack() as ctx:
         const = ctx.enter_context(tc.tile_pool(name="const", bufs=1))
-        w_raw_pool = ctx.enter_context(tc.tile_pool(name="w_raw", bufs=AHEAD + 1))
+        w_raw_pool = ctx.enter_context(tc.tile_pool(name="w_raw", bufs=STEP_BLOCKS * (AHEAD + 1)))
         c_raw_pool = ctx.enter_context(tc.tile_pool(name="c_raw", bufs=STEP_PASSES * (AHEAD + 1)))
-        w_grouped_pool = ctx.enter_context(tc.tile_pool(name="w_grouped", bufs=3))
+        w_grouped_pool = ctx.enter_context(tc.tile_pool(name="w_grouped", bufs=4))
         c_grouped_pool = ctx.enter_context(tc.tile_pool(name="c_grouped", bufs=4))
-        w_mx_pool = ctx.enter_context(tc.tile_pool(name="w_mx", bufs=SLABS))
+        w_mx_pool = ctx.enter_context(tc.tile_pool(name="w_mx", bufs=12))
         c_mx_pool = ctx.enter_context(tc.tile_pool(name="c_mx", bufs=6))
         result_pool = ctx.enter_context(tc.tile_pool(name="result", bufs=O_TILES))
         acc_pool = ctx.enter_context(tc.psum_pool(name="acc", bufs=O_TILES))
@@ -56,6 +56,117 @@ def tile_block_height_reducing_filtering_pb_k_kernel(tc, head_res, W_merge, g_m,
         w_raws, w_groupeds, w_codes, w_scales = {}, {}, {}, {}
         c_raws, c_groupeds, c_codes, c_scales = {}, {}, {}, {}
 
+        acc = []
+        for t in range(O_TILES):
+            acc_t = acc_pool.tile([P, COLUMNS], F32, tag="acc")
+            acc.append(acc_t)
+
+        def load_block(c, t, parts):
+            w_raw = w_raw_pool.tile([P, BLOCK_PASSES * K_PASS], BF16)
+            w_raws[c, t] = w_raw
+            width = BLOCK_PASSES * K_PASS // parts
+            for h in range(parts):
+                k0 = c * BLOCK_PASSES * K_PASS + h * width
+                nc.sync.dma_start(
+                    out=w_raw[:, h * width : (h + 1) * width], in_=W_merge[t * P : (t + 1) * P, k0 : k0 + width]
+                )
+
+        def load_pass(q):
+            n, g = divmod(q, CHANNELS // K_PASS)
+            c_raw = c_raw_pool.tile([P, SAMPLES, PACK * POSITIONS], BF16)
+            rows = head_res[n, :, g * K_PASS : (g + 1) * K_PASS, :]
+            nc.sync.dma_start(out=c_raw[:], in_=rows.rearrange("b (p j) w -> p b (j w)", j=PACK))
+            c_raws[q] = c_raw
+
+        def transpose_bank(c, t, h):
+            words = w_raws[c, t][:].bitcast(F32).rearrange("o (g p s) -> o g s p", p=P, s=PAIR)
+            wt = wt_pool.tile([P, BANK_PASSES, PAIR, P], F32)
+            for i in range(BANK_PASSES):
+                for s in range(PAIR):
+                    nc.tensor.transpose(wt[:, i, s, :], words[:, h * BANK_PASSES + i, s, :], ident[:])
+            return wt
+
+        def empty_bank(copy, c, t, h, wt):
+            if h == 0:
+                w_grouped = w_grouped_pool.tile([P, BLOCK_PASSES, P, PACK], BF16, align_bytes=64)
+                w_groupeds[c, t] = w_grouped
+            words = w_groupeds[c, t][:].bitcast(F32)
+            copy(
+                out=words[:, h * BANK_PASSES : (h + 1) * BANK_PASSES],
+                in_=wt[:].rearrange("p g s o -> p g o s"),
+            )
+
+        def quantise_block(c, t, h0, h1):
+            if h0 == 0:
+                w_code = w_mx_pool.tile([P, BLOCK_BANKS * BANK_WORDS], U32, align_bytes=64)
+                w_scale = w_mx_pool.tile([P, BLOCK_BANKS * BANK_WORDS], U8, align_bytes=64)
+                w_codes[c, t], w_scales[c, t] = w_code, w_scale
+            cols = slice(h0 * BANK_WORDS, h1 * BANK_WORDS)
+            nc.vector.quantize_mx(
+                out=w_codes[c, t][:, cols].bitcast(FP8X4),
+                scales=w_scales[c, t][:, cols],
+                in_=w_groupeds[c, t][:, h0 * BANK_PASSES : h1 * BANK_PASSES].rearrange("p g o t -> p (g o t)"),
+            )
+
+        def regroup_views(q):
+            src = c_raws[q][:].rearrange("p b (t c i) -> p c b t i", t=PACK, i=RUN)
+            dst = c_groupeds[q][:].rearrange("p (b c i) t -> p c b t i", b=SAMPLES, i=RUN)
+            return dst, src
+
+        def regroup_pass(q, vector_groups):
+            c_grouped = c_grouped_pool.tile([P, COLUMNS, PACK], BF16, align_bytes=64)
+            c_groupeds[q] = c_grouped
+            dst, src = regroup_views(q)
+            nc.vector.tensor_copy(out=dst[:, 0:vector_groups], in_=src[:, 0:vector_groups])
+            nc.scalar.copy(out=dst[:, vector_groups:GROUPS], in_=src[:, vector_groups:GROUPS])
+
+        def quantise_pass(q):
+            c_code = c_mx_pool.tile([P, COLUMNS], U32, align_bytes=64)
+            c_scale = c_mx_pool.tile([P, COLUMNS], U8, align_bytes=64)
+            c_codes[q], c_scales[q] = c_code, c_scale
+            nc.vector.quantize_mx(
+                out=c_code[:].bitcast(FP8X4),
+                scales=c_scale[:],
+                in_=c_groupeds[q][:].rearrange("p c t -> p (c t)"),
+            )
+
+        def multiply(q, t):
+            c, g = divmod(q, BLOCK_PASSES)
+            cols = slice(g * P, (g + 1) * P)
+            nc.tensor.matmul_mx(
+                out=acc[t][:],
+                lhsT=w_codes[c, t][:, cols].bitcast(FP8X4),
+                lhsT_scale=w_scales[c, t][:, cols],
+                rhs=c_codes[q][:].bitcast(FP8X4),
+                rhs_scale=c_scales[q][:],
+                start=(q == 0),
+                stop=(q == PASSES - 1),
+            )
+
+        last = (CHUNKS - 1, O_TILES - 1)
+
+        def step_blocks(i):
+            if not 0 <= i < STEPS:
+                return []
+            blocks = [divmod(STEP_BLOCKS * i + j, O_TILES) for j in range(STEP_BLOCKS)]
+            return [block for block in blocks if block != last]
+
+        def step_passes(i):
+            q = STEP_PASSES * (i - 1)
+            return [q, q + 1] if 0 <= q < PASSES else []
+
+        def load_step(i):
+            blocks, passes = step_blocks(i), step_passes(i)
+            for j in range(STEP_PASSES):
+                if j < len(blocks):
+                    load_block(*blocks[j], 1)
+                if j < len(passes):
+                    load_pass(passes[j])
+            if i == STEPS + 1:
+                load_block(*last, BLOCK_BANKS)
+
+        for i in range(2):
+            load_step(i)
         gb_rows = const.tile([P, P], BF16)
         nc.vector.memset(gb_rows[:], 0.0)
         nc.scalar.dma_start(out=gb_rows[0:O_TILES, :], in_=g_m.rearrange("(t o) -> t o", o=P))
@@ -66,129 +177,33 @@ def tile_block_height_reducing_filtering_pb_k_kernel(tc, head_res, W_merge, g_m,
         make_identity(nc, ident_bf16[:])
         eps = const.tile([P, 1], F32)
         nc.vector.memset(eps[:], EPS)
-        first_sqrt = const.tile([P, 1], F32)
-        nc.scalar.activation(out=first_sqrt[:], in_=eps[:], func=ACT.Sqrt)
+        first_root = const.tile([P, 1], F32)
+        nc.scalar.activation(out=first_root[:], in_=eps[:], func=ACT.Abs_reciprocal_sqrt)
+        for i in range(2, AHEAD):
+            load_step(i)
 
-        acc = []
-        for t in range(O_TILES):
-            acc_t = acc_pool.tile([P, COLUMNS], F32, tag="acc")
-            acc.append(acc_t)
-
-        def load_slab(u):
-            if not 0 <= u < SLABS:
-                return
-            n, t = divmod(u, O_TILES)
-            w_raw = w_raw_pool.tile([P, CHANNELS], BF16)
-            nc.sync.dma_start(
-                out=w_raw[:], in_=W_merge[t * P : (t + 1) * P, n * CHANNELS : (n + 1) * CHANNELS]
-            )
-            w_raws[u] = w_raw
-
-        def load_pass(q):
-            if not 0 <= q < PASSES:
-                return
-            n, g = divmod(q, HEAD_PASSES)
-            c_raw = c_raw_pool.tile([P, SAMPLES, PACK * POSITIONS], BF16)
-            rows = head_res[n, :, g * K_PASS : (g + 1) * K_PASS, :]
-            nc.sync.dma_start(out=c_raw[:], in_=rows.rearrange("b (p j) w -> p b (j w)", j=PACK))
-            c_raws[q] = c_raw
-
-        def transpose_half_slab(u, half):
-            if not 0 <= u < SLABS:
-                return
-            if half == 0:
-                w_grouped = w_grouped_pool.tile([P, HEAD_PASSES, P, PACK], BF16, align_bytes=64)
-                w_groupeds[u] = w_grouped
-            words = w_raws[u][:].bitcast(F32).rearrange("o (g p s) -> o g s p", p=P, s=PAIR)
-            grouped_words = w_groupeds[u][:].bitcast(F32)
-            first = half * HALF_PASSES
-            for g0 in range(first, first + HALF_PASSES, BANK_PASSES):
-                wt = wt_pool.tile([P, BANK_PASSES, PAIR, P], F32)
-                for i in range(BANK_PASSES):
-                    for s in range(PAIR):
-                        nc.tensor.transpose(wt[:, i, s, :], words[:, g0 + i, s, :], ident[:])
-                nc.scalar.copy(
-                    out=grouped_words[:, g0 : g0 + BANK_PASSES, :, :],
-                    in_=wt[:].rearrange("p g s o -> p g o s"),
-                )
-
-        def quantise_half_slab(u, half):
-            if not 0 <= u < SLABS:
-                return
-            if half == 0:
-                w_code = w_mx_pool.tile([P, HEAD_PASSES * P], U32, align_bytes=64)
-                w_scale = w_mx_pool.tile([P, HEAD_PASSES * P], U8, align_bytes=64)
-                w_codes[u], w_scales[u] = w_code, w_scale
-            passes = slice(half * HALF_PASSES, (half + 1) * HALF_PASSES)
-            cols = slice(half * HALF_WORDS, (half + 1) * HALF_WORDS)
-            nc.vector.quantize_mx(
-                out=w_codes[u][:, cols].bitcast(FP8X4),
-                scales=w_scales[u][:, cols],
-                in_=w_groupeds[u][:, passes, :, :].rearrange("p g o t -> p (g o t)"),
-            )
-
-        def regroup_pass(q):
-            if not 0 <= q < PASSES:
-                return
-            c_grouped = c_grouped_pool.tile([P, COLUMNS, PACK], BF16, align_bytes=64)
-            c_groupeds[q] = c_grouped
-            src = c_raws[q][:].rearrange("p b (t c i) -> p c b t i", t=PACK, i=RUN)
-            dst = c_grouped[:].rearrange("p (b c i) t -> p c b t i", b=SAMPLES, i=RUN)
-            scalar_samples = 1 if q // STEP_PASSES + LEAD < SLABS else 2
-            vector_samples = SAMPLES - scalar_samples
-            nc.vector.tensor_copy(out=dst[:, :, 0:vector_samples], in_=src[:, :, 0:vector_samples])
-            for b in range(vector_samples, SAMPLES):
-                nc.scalar.copy(out=dst[:, :, b], in_=src[:, :, b])
-
-        def quantise_pass(q):
-            if not 0 <= q < PASSES:
-                return
-            c_code = c_mx_pool.tile([P, COLUMNS], U32, align_bytes=64)
-            c_scale = c_mx_pool.tile([P, COLUMNS], U8, align_bytes=64)
-            c_codes[q], c_scales[q] = c_code, c_scale
-            nc.vector.quantize_mx(
-                out=c_code[:].bitcast(FP8X4),
-                scales=c_scale[:],
-                in_=c_groupeds[q][:].rearrange("p c t -> p (c t)"),
-            )
-
-        def multiply_pass(q):
-            if not 0 <= q < PASSES:
-                return
-            n, g = divmod(q, HEAD_PASSES)
-            cols = slice(g * P, (g + 1) * P)
-            for t in range(O_TILES):
-                u = n * O_TILES + t
-                nc.tensor.matmul_mx(
-                    out=acc[t][:],
-                    lhsT=w_codes[u][:, cols].bitcast(FP8X4),
-                    lhsT_scale=w_scales[u][:, cols],
-                    rhs=c_codes[q][:].bitcast(FP8X4),
-                    rhs_scale=c_scales[q][:],
-                    start=(q == 0),
-                    stop=(q == PASSES - 1),
-                )
-
-        def load_step(s):
-            load_slab(s)
-            load_pass(STEP_PASSES * (s - LEAD))
-            load_pass(STEP_PASSES * (s - LEAD) + 1)
-
-        for s in range(AHEAD):
-            load_step(s)
-        for s in range(STEPS + DRAIN):
-            q = STEP_PASSES * (s - LEAD)
-            load_step(s + AHEAD)
-            transpose_half_slab(s, 0)
-            regroup_pass(q)
-            transpose_half_slab(s, 1)
-            multiply_pass(q - 3)
-            multiply_pass(q - 2)
-            quantise_half_slab(s - 1, 0)
-            quantise_pass(q - 1)
-            regroup_pass(q + 1)
-            quantise_half_slab(s - 1, 1)
-            quantise_pass(q)
+        for i in range(STEPS + 1):
+            load_step(i + AHEAD)
+            blocks, passes = step_blocks(i), step_passes(i)
+            ready_blocks, ready_passes = step_blocks(i - 1), step_passes(i - 1)
+            vector_groups = (16, 20, 22)[len(blocks)]
+            for j in range(STEP_BLOCKS):
+                if j < len(blocks):
+                    banks = [transpose_bank(*blocks[j], h) for h in range(BLOCK_BANKS)]
+                    for h in range(BLOCK_BANKS):
+                        empty_bank(nc.scalar.copy, *blocks[j], h, banks[h])
+                if j < len(ready_blocks):
+                    quantise_block(*ready_blocks[j], 0, BLOCK_BANKS)
+                if j == 1 and ready_passes:
+                    quantise_pass(ready_passes[1])
+                if passes:
+                    regroup_pass(passes[j], vector_groups)
+            if passes:
+                quantise_pass(passes[0])
+            for q in ready_passes:
+                for t in range(O_TILES):
+                    if (q // BLOCK_PASSES, t) != last:
+                        multiply(q, t)
 
         gb_bank = wt_pool.tile([P, P], BF16, tag="wt")
         nc.tensor.transpose(gb_bank[:], gb_rows[:], ident_bf16[:])
@@ -196,42 +211,66 @@ def tile_block_height_reducing_filtering_pb_k_kernel(tc, head_res, W_merge, g_m,
         nc.scalar.copy(out=gb[:], in_=gb_bank[:, 0 : 2 * O_TILES])
         g_cols, b_cols = gb[:, 0:O_TILES], gb[:, O_TILES : 2 * O_TILES]
 
+        quantise_pass(PASSES - 1)
+        banks = [transpose_bank(*last, h) for h in range(BLOCK_BANKS)]
+        empty_bank(nc.scalar.copy, *last, 0, banks[0])
+        empty_bank(nc.vector.tensor_copy, *last, 1, banks[1])
+        for t in range(O_TILES - 1):
+            for q in range(PASSES - STEP_PASSES, PASSES):
+                multiply(q, t)
+        quantise_block(*last, 0, 1)
+        quantise_block(*last, 1, 2)
+        for q in range(PASSES - BLOCK_PASSES, PASSES):
+            multiply(q, O_TILES - 1)
+
         stats = const.tile([P, O_TILES, 6], F32)
         mean_var = const.tile([P, O_TILES, 2], F32)
-        for t in range(O_TILES):
-            nc.vector.bn_stats(out=stats[:, t, :], in_=acc[t][:])
-            nc.vector.bn_aggr(out=mean_var[:, t, :], in_=stats[:, t, :])
-        mean, var = mean_var[:, :, 0], mean_var[:, :, 1]
-        std = const.tile([P, O_TILES], F32)
-        nc.scalar.activation(out=std[:], in_=var, func=ACT.Sqrt, bias=eps[:, 0:1], scale=1.0)
-        mean_g = const.tile([P, O_TILES], F32)
-        nc.vector.tensor_mul(out=mean_g[:], in0=mean, in1=g_cols)
         inv_std = const.tile([P, O_TILES], F32)
-        nc.vector.reciprocal(out=inv_std[:], in_=std[:])
         gain = const.tile([P, O_TILES], F32)
-        nc.vector.tensor_mul(out=gain[:], in0=g_cols, in1=inv_std[:])
-        mean_gain = const.tile([P, O_TILES], F32)
-        nc.vector.tensor_mul(out=mean_gain[:], in0=mean_g[:], in1=inv_std[:])
+        minus_mean_g = const.tile([P, O_TILES], F32)
         shift = const.tile([P, O_TILES], F32)
-        nc.vector.tensor_sub(out=shift[:], in0=b_cols, in1=mean_gain[:])
-
         results = []
         for t in range(O_TILES):
             result = result_pool.tile([P, COLUMNS], F32)
             results.append(result)
 
-        def store(t):
-            nc.sync.dma_start(
-                out=out[:, t * P : (t + 1) * P, :].rearrange("b o d -> o b d"),
-                in_=results[t][:].rearrange("o (b d) -> o b d", b=SAMPLES),
+        def find_stats(t):
+            nc.vector.bn_stats(out=stats[:, t, :], in_=acc[t][:])
+
+        def find_mean_var(t):
+            nc.vector.bn_aggr(out=mean_var[:, t, :], in_=stats[:, t, :])
+
+        def find_inv_std(t0, t1):
+            nc.scalar.activation(
+                out=inv_std[:, t0:t1], in_=mean_var[:, t0:t1, 1], func=ACT.Abs_reciprocal_sqrt, bias=eps[:, 0:1], scale=1.0
             )
 
-        for t in range(0, O_TILES, 2):
+        def find_gain_shift(t0, t1):
+            nc.vector.scalar_tensor_tensor(
+                out=minus_mean_g[:, t0:t1],
+                in0=mean_var[:, t0:t1, 0],
+                scalar=-1.0,
+                in1=g_cols[:, t0:t1],
+                op0=ALU.mult,
+                op1=ALU.mult,
+            )
+            nc.vector.tensor_mul(out=gain[:, t0:t1], in0=g_cols[:, t0:t1], in1=inv_std[:, t0:t1])
+            for t in range(t0, t1):
+                nc.vector.scalar_tensor_tensor(
+                    out=shift[:, t : t + 1],
+                    in0=minus_mean_g[:, t : t + 1],
+                    scalar=inv_std[:, t : t + 1],
+                    in1=b_cols[:, t : t + 1],
+                    op0=ALU.mult,
+                    op1=ALU.add,
+                )
+
+        def scalar_relu(t):
             nc.scalar.activation(
                 out=results[t][:], in_=acc[t][:], func=ACT.Relu, bias=shift[:, t : t + 1], scale=gain[:, t : t + 1]
             )
-            store(t)
-        for t in range(1, O_TILES, 2):
+
+        def vector_relu(t):
             nc.vector.tensor_scalar(
                 out=results[t][:],
                 in0=acc[t][:],
@@ -240,6 +279,31 @@ def tile_block_height_reducing_filtering_pb_k_kernel(tc, head_res, W_merge, g_m,
                 op0=ALU.mult,
                 op1=ALU.add,
             )
-        for t in range(1, O_TILES, 2):
             nc.vector.tensor_scalar_max(out=results[t][:], in0=results[t][:], scalar1=0.0)
-            store(t)
+
+        def store(t):
+            nc.sync.dma_start(
+                out=out[:, t * P : (t + 1) * P, :].rearrange("b o d -> o b d"),
+                in_=results[t][:].rearrange("o (b d) -> o b d", b=SAMPLES),
+            )
+
+        find_stats(0)
+        find_stats(1)
+        find_mean_var(0)
+        find_mean_var(1)
+        find_inv_std(0, 2)
+        find_stats(2)
+        find_gain_shift(0, 2)
+        find_mean_var(2)
+        scalar_relu(0)
+        store(0)
+        find_stats(3)
+        find_mean_var(3)
+        find_inv_std(2, 4)
+        scalar_relu(1)
+        store(1)
+        find_gain_shift(2, 4)
+        scalar_relu(3)
+        store(3)
+        vector_relu(2)
+        store(2)

@@ -187,23 +187,23 @@ def tile_block_height_reducing_filtering_pb_k_kernel(tc, head_res, W_merge, g_m,
             blocks, passes = step_blocks(i), step_passes(i)
             ready_blocks, ready_passes = step_blocks(i - 1), step_passes(i - 1)
             vector_groups = (16, 20, 22)[len(blocks)]
+            for block in ready_blocks:
+                quantise_block(*block, 0, BLOCK_BANKS)
             for j in range(STEP_BLOCKS):
                 if j < len(blocks):
                     banks = [transpose_bank(*blocks[j], h) for h in range(BLOCK_BANKS)]
                     for h in range(BLOCK_BANKS):
                         empty_bank(nc.scalar.copy, *blocks[j], h, banks[h])
-                if j < len(ready_blocks):
-                    quantise_block(*ready_blocks[j], 0, BLOCK_BANKS)
                 if j == 1 and ready_passes:
                     quantise_pass(ready_passes[1])
                 if passes:
                     regroup_pass(passes[j], vector_groups)
+                if ready_passes:
+                    for t in range(O_TILES):
+                        if (ready_passes[j] // BLOCK_PASSES, t) != last:
+                            multiply(ready_passes[j], t)
             if passes:
                 quantise_pass(passes[0])
-            for q in ready_passes:
-                for t in range(O_TILES):
-                    if (q // BLOCK_PASSES, t) != last:
-                        multiply(q, t)
 
         gb_bank = wt_pool.tile([P, P], BF16, tag="wt")
         nc.tensor.transpose(gb_bank[:], gb_rows[:], ident_bf16[:])

@@ -42,7 +42,7 @@ def tile_block_height_reducing_filtering_pb_k_kernel(tc, head_res, W_merge, g_m,
     nc = tc.nc
     with ExitStack() as ctx:
         const = ctx.enter_context(tc.tile_pool(name="const", bufs=1))
-        w_raw_pool = ctx.enter_context(tc.tile_pool(name="w_raw", bufs=STEP_BLOCKS * (AHEAD + 1)))
+        w_raw_pool = ctx.enter_context(tc.tile_pool(name="w_raw", bufs=AHEAD + 1))
         c_raw_pool = ctx.enter_context(tc.tile_pool(name="c_raw", bufs=STEP_PASSES * (AHEAD + 1)))
         w_grouped_pool = ctx.enter_context(tc.tile_pool(name="w_grouped", bufs=4))
         c_grouped_pool = ctx.enter_context(tc.tile_pool(name="c_grouped", bufs=4))
@@ -61,14 +61,18 @@ def tile_block_height_reducing_filtering_pb_k_kernel(tc, head_res, W_merge, g_m,
             acc_t = acc_pool.tile([P, COLUMNS], F32, tag="acc")
             acc.append(acc_t)
 
-        def load_block(c, t, parts):
-            w_raw = w_raw_pool.tile([P, BLOCK_PASSES * K_PASS], BF16)
-            w_raws[c, t] = w_raw
+        def load_blocks(blocks, parts):
+            c, t0 = blocks[0]
+            w_raw = w_raw_pool.tile([P, STEP_BLOCKS, BLOCK_PASSES * K_PASS], BF16)
+            for j in range(len(blocks)):
+                w_raws[c, t0 + j] = w_raw[:, j]
             width = BLOCK_PASSES * K_PASS // parts
             for h in range(parts):
                 k0 = c * BLOCK_PASSES * K_PASS + h * width
+                rows = W_merge[t0 * P : (t0 + len(blocks)) * P, k0 : k0 + width]
                 nc.sync.dma_start(
-                    out=w_raw[:, h * width : (h + 1) * width], in_=W_merge[t * P : (t + 1) * P, k0 : k0 + width]
+                    out=w_raw[:, 0 : len(blocks), h * width : (h + 1) * width],
+                    in_=rows.rearrange("(t o) k -> o t k", o=P),
                 )
 
         def load_pass(q):
@@ -79,7 +83,7 @@ def tile_block_height_reducing_filtering_pb_k_kernel(tc, head_res, W_merge, g_m,
             c_raws[q] = c_raw
 
         def transpose_bank(c, t, h):
-            words = w_raws[c, t][:].bitcast(F32).rearrange("o (g p s) -> o g s p", p=P, s=PAIR)
+            words = w_raws[c, t].bitcast(F32).rearrange("o (g p s) -> o g s p", p=P, s=PAIR)
             wt = wt_pool.tile([P, BANK_PASSES, PAIR, P], F32)
             for i in range(BANK_PASSES):
                 for s in range(PAIR):
@@ -157,13 +161,12 @@ def tile_block_height_reducing_filtering_pb_k_kernel(tc, head_res, W_merge, g_m,
 
         def load_step(i):
             blocks, passes = step_blocks(i), step_passes(i)
-            for j in range(STEP_PASSES):
-                if j < len(blocks):
-                    load_block(*blocks[j], 1)
-                if j < len(passes):
-                    load_pass(passes[j])
+            if blocks:
+                load_blocks(blocks, 1)
+            for q in passes:
+                load_pass(q)
             if i == STEPS + 1:
-                load_block(*last, BLOCK_BANKS)
+                load_blocks([last], BLOCK_BANKS)
 
         for i in range(2):
             load_step(i)

@@ -113,16 +113,16 @@ def tile_block_height_reducing_filtering_pb_k_kernel(tc, head_res, W_merge, g_m,
             )
 
         def regroup_views(q):
-            src = c_raws[q][:].rearrange("p b (t c i) -> p c b t i", t=PACK, i=RUN)
-            dst = c_groupeds[q][:].rearrange("p (b c i) t -> p c b t i", b=SAMPLES, i=RUN)
+            src = c_raws[q][:].rearrange("p b (t c i) -> p b c t i", t=PACK, i=RUN)
+            dst = c_groupeds[q][:].rearrange("p (b c i) t -> p b c t i", b=SAMPLES, i=RUN)
             return dst, src
 
         def regroup_pass(q, vector_groups):
             c_grouped = c_grouped_pool.tile([P, COLUMNS, PACK], BF16, align_bytes=64)
             c_groupeds[q] = c_grouped
             dst, src = regroup_views(q)
-            nc.vector.tensor_copy(out=dst[:, 0:vector_groups], in_=src[:, 0:vector_groups])
-            nc.scalar.copy(out=dst[:, vector_groups:GROUPS], in_=src[:, vector_groups:GROUPS])
+            nc.vector.tensor_copy(out=dst[:, :, 0:vector_groups], in_=src[:, :, 0:vector_groups])
+            nc.scalar.copy(out=dst[:, :, vector_groups:GROUPS], in_=src[:, :, vector_groups:GROUPS])
 
         def quantise_pass(q):
             c_code = c_mx_pool.tile([P, COLUMNS], U32, align_bytes=64)

@@ -159,21 +159,30 @@ def tile_block_height_reducing_filtering_pb_k_kernel(tc, head_res, W_merge, g_m,
             q = STEP_PASSES * (i - 1)
             return [q, q + 1] if 0 <= q < PASSES else []
 
+        first, second, third, fourth = range(PASSES - BLOCK_PASSES, PASSES)
+        late = (CHUNKS - 1, O_TILES - 2)
+
         def load_step(i):
-            blocks, passes = step_blocks(i), step_passes(i)
-            if blocks:
-                load_blocks(blocks, 1)
-            for q in passes:
-                load_pass(q)
-            if i == STEPS + 1:
+            if i < STEPS - 1:
+                if step_blocks(i):
+                    load_blocks(step_blocks(i), 1)
+                for q in step_passes(i):
+                    load_pass(q)
+            elif i == STEPS - 1:
+                load_blocks([late], 1)
+                load_pass(first)
+                load_pass(second)
+            elif i == STEPS:
+                load_pass(third)
+                load_pass(fourth)
                 load_blocks([last], BLOCK_BANKS)
 
-        for i in range(2):
-            load_step(i)
         gb_rows = const.tile([P, P], BF16)
         nc.vector.memset(gb_rows[:], 0.0)
         nc.scalar.dma_start(out=gb_rows[0:O_TILES, :], in_=g_m.rearrange("(t o) -> t o", o=P))
         nc.scalar.dma_start(out=gb_rows[O_TILES : 2 * O_TILES, :], in_=b_m.rearrange("(t o) -> t o", o=P))
+        for i in range(2):
+            load_step(i)
         ident = const.tile([P, P], F32)
         make_identity(nc, ident[:])
         ident_bf16 = const.tile([P, P], BF16)
@@ -185,11 +194,17 @@ def tile_block_height_reducing_filtering_pb_k_kernel(tc, head_res, W_merge, g_m,
         for i in range(2, AHEAD):
             load_step(i)
 
-        for i in range(STEPS + 1):
+        for i in range(STEPS - 1):
+            if i == 3:
+                gb_bank = wt_pool.tile([P, P], BF16, tag="wt")
+                nc.tensor.transpose(gb_bank[:], gb_rows[:], ident_bf16[:])
+                gb = const.tile([P, 2 * O_TILES], F32)
+                nc.scalar.copy(out=gb[:], in_=gb_bank[:, 0 : 2 * O_TILES])
+                g_cols, b_cols = gb[:, 0:O_TILES], gb[:, O_TILES : 2 * O_TILES]
             load_step(i + AHEAD)
             blocks, passes = step_blocks(i), step_passes(i)
             ready_blocks, ready_passes = step_blocks(i - 1), step_passes(i - 1)
-            vector_groups = (16, 20, 22)[len(blocks)]
+            vector_groups = 22
             for block in ready_blocks:
                 quantise_block(*block, 0, BLOCK_BANKS)
             for j in range(STEP_BLOCKS):
@@ -208,29 +223,44 @@ def tile_block_height_reducing_filtering_pb_k_kernel(tc, head_res, W_merge, g_m,
             if passes:
                 quantise_pass(passes[0])
 
-        gb_bank = wt_pool.tile([P, P], BF16, tag="wt")
-        nc.tensor.transpose(gb_bank[:], gb_rows[:], ident_bf16[:])
-        gb = const.tile([P, 2 * O_TILES], F32)
-        nc.scalar.copy(out=gb[:], in_=gb_bank[:, 0 : 2 * O_TILES])
-        g_cols, b_cols = gb[:, 0:O_TILES], gb[:, O_TILES : 2 * O_TILES]
-
-        quantise_pass(PASSES - 1)
-        banks = [transpose_bank(*last, h) for h in range(BLOCK_BANKS)]
-        empty_bank(nc.scalar.copy, *last, 0, banks[0])
-        empty_bank(nc.vector.tensor_copy, *last, 1, banks[1])
-        for t in range(O_TILES - 1):
-            for q in range(PASSES - STEP_PASSES, PASSES):
+        def multiply_early_tiles(q):
+            for t in range(O_TILES - 1):
                 multiply(q, t)
-        quantise_block(*last, 0, 1)
-        quantise_block(*last, 1, 2)
-        for q in range(PASSES - BLOCK_PASSES, PASSES):
-            multiply(q, O_TILES - 1)
 
+        for block in step_blocks(STEPS - 2):
+            quantise_block(*block, 0, BLOCK_BANKS)
+        banks = [transpose_bank(*late, h) for h in range(BLOCK_BANKS)]
+        regroup_pass(first, 20)
+        for t in range(O_TILES):
+            multiply(first - 2, t)
+        for h in range(BLOCK_BANKS):
+            empty_bank(nc.scalar.copy, *late, h, banks[h])
+        quantise_pass(first - 1)
+        regroup_pass(second, 20)
+        quantise_pass(first)
+        for t in range(O_TILES):
+            multiply(first - 1, t)
+        quantise_block(*late, 0, BLOCK_BANKS)
+        quantise_pass(second)
+        regroup_pass(third, 18)
+        multiply_early_tiles(first)
+        multiply_early_tiles(second)
+        banks = [transpose_bank(*last, h) for h in range(BLOCK_BANKS)]
+        regroup_pass(fourth, 18)
+        quantise_pass(third)
+        quantise_pass(fourth)
+        for h in range(BLOCK_BANKS):
+            empty_bank(nc.scalar.copy, *last, h, banks[h])
+        for t in range(O_TILES - 1):
+            multiply(third, t)
+            multiply(fourth, t)
         stats = const.tile([P, O_TILES, 6], F32)
         mean_var = const.tile([P, O_TILES, 2], F32)
         inv_std = const.tile([P, O_TILES], F32)
         gain = const.tile([P, O_TILES], F32)
-        minus_mean_g = const.tile([P, O_TILES], F32)
+        early_gain = const.tile([P, 2], F32)
+        early_shift = const.tile([P, 2], F32)
+        minus_mean_g = const.tile([P, 1], F32)
         shift = const.tile([P, O_TILES], F32)
         results = []
         for t in range(O_TILES):
@@ -243,46 +273,65 @@ def tile_block_height_reducing_filtering_pb_k_kernel(tc, head_res, W_merge, g_m,
         def find_mean_var(t):
             nc.vector.bn_aggr(out=mean_var[:, t, :], in_=stats[:, t, :])
 
-        def find_inv_std(t0, t1):
+        def find_inv_std(t):
             nc.scalar.activation(
-                out=inv_std[:, t0:t1], in_=mean_var[:, t0:t1, 1], func=ACT.Abs_reciprocal_sqrt, bias=eps[:, 0:1], scale=1.0
+                out=inv_std[:, t : t + 1],
+                in_=mean_var[:, t, 1:2],
+                func=ACT.Abs_reciprocal_sqrt,
+                bias=eps[:, 0:1],
+                scale=1.0,
             )
 
-        def find_gain_shift(t0, t1):
+        def find_gain(t):
+            nc.vector.tensor_mul(out=gain[:, t : t + 1], in0=g_cols[:, t : t + 1], in1=inv_std[:, t : t + 1])
+
+        def find_minus_mean_g(t):
             nc.vector.scalar_tensor_tensor(
-                out=minus_mean_g[:, t0:t1],
-                in0=mean_var[:, t0:t1, 0],
+                out=minus_mean_g[:],
+                in0=mean_var[:, t, 0:1],
                 scalar=-1.0,
-                in1=g_cols[:, t0:t1],
+                in1=g_cols[:, t : t + 1],
                 op0=ALU.mult,
                 op1=ALU.mult,
             )
-            nc.vector.tensor_mul(out=gain[:, t0:t1], in0=g_cols[:, t0:t1], in1=inv_std[:, t0:t1])
-            for t in range(t0, t1):
-                nc.vector.scalar_tensor_tensor(
-                    out=shift[:, t : t + 1],
-                    in0=minus_mean_g[:, t : t + 1],
-                    scalar=inv_std[:, t : t + 1],
-                    in1=b_cols[:, t : t + 1],
-                    op0=ALU.mult,
-                    op1=ALU.add,
-                )
+
+        def find_shift(t):
+            nc.vector.scalar_tensor_tensor(
+                out=shift[:, t : t + 1],
+                in0=minus_mean_g[:],
+                scalar=inv_std[:, t : t + 1],
+                in1=b_cols[:, t : t + 1],
+                op0=ALU.mult,
+                op1=ALU.add,
+            )
+
+        def find_gain_shift_on_gpsimd(t):
+            mean_gain = const.tile([P, 1], F32, name="mean_gain")
+            nc.gpsimd.tensor_mul(out=early_gain[:, t : t + 1], in0=g_cols[:, t : t + 1], in1=inv_std[:, t : t + 1])
+            nc.gpsimd.tensor_mul(out=mean_gain[:], in0=mean_var[:, t, 0:1], in1=early_gain[:, t : t + 1])
+            nc.gpsimd.tensor_sub(out=early_shift[:, t : t + 1], in0=b_cols[:, t : t + 1], in1=mean_gain[:])
 
         def scalar_relu(t):
             nc.scalar.activation(
-                out=results[t][:], in_=acc[t][:], func=ACT.Relu, bias=shift[:, t : t + 1], scale=gain[:, t : t + 1]
+                out=results[t][:],
+                in_=acc[t][:],
+                func=ACT.Relu,
+                bias=(early_shift if t < 2 else shift)[:, t : t + 1],
+                scale=(early_gain if t < 2 else gain)[:, t : t + 1],
             )
 
         def vector_relu(t):
             nc.vector.tensor_scalar(
                 out=results[t][:],
                 in0=acc[t][:],
-                scalar1=gain[:, t : t + 1],
-                scalar2=shift[:, t : t + 1],
-                op0=ALU.mult,
-                op1=ALU.add,
+                scalar1=mean_var[:, t, 0:1],
+                scalar2=gain[:, t : t + 1],
+                op0=ALU.subtract,
+                op1=ALU.mult,
             )
-            nc.vector.tensor_scalar_max(out=results[t][:], in0=results[t][:], scalar1=0.0)
+            nc.vector.tensor_scalar(
+                out=results[t][:], in0=results[t][:], scalar1=b_cols[:, t : t + 1], scalar2=0.0, op0=ALU.add, op1=ALU.max
+            )
 
         def store(t):
             nc.sync.dma_start(
@@ -290,22 +339,32 @@ def tile_block_height_reducing_filtering_pb_k_kernel(tc, head_res, W_merge, g_m,
                 in_=results[t][:].rearrange("o (b d) -> o b d", b=SAMPLES),
             )
 
+        quantise_block(*last, 0, 1)
+        quantise_block(*last, 1, 2)
         find_stats(0)
-        find_stats(1)
+        for q in (first, second, third, fourth):
+            multiply(q, O_TILES - 1)
         find_mean_var(0)
+        find_inv_std(0)
+        find_gain_shift_on_gpsimd(0)
+        find_stats(1)
         find_mean_var(1)
-        find_inv_std(0, 2)
-        find_stats(2)
-        find_gain_shift(0, 2)
-        find_mean_var(2)
+        find_inv_std(1)
         scalar_relu(0)
         store(0)
+        find_gain_shift_on_gpsimd(1)
+        find_stats(2)
         find_stats(3)
+        find_mean_var(2)
         find_mean_var(3)
-        find_inv_std(2, 4)
         scalar_relu(1)
         store(1)
-        find_gain_shift(2, 4)
+        find_inv_std(2)
+        find_inv_std(3)
+        find_minus_mean_g(3)
+        find_gain(2)
+        find_gain(3)
+        find_shift(3)
         scalar_relu(3)
         store(3)
         vector_relu(2)

@@ -31,6 +31,7 @@ CHUNKS = PASSES // BLOCK_PASSES
 STEP_BLOCKS = 2
 STEP_PASSES = 2
 STEPS = CHUNKS * O_TILES // STEP_BLOCKS
+SLAB_STEPS = (HEADS - 1) * O_TILES
 AHEAD = 6
 RUN = 4
 GROUPS = POSITIONS // RUN
@@ -46,8 +47,8 @@ def tile_block_height_reducing_filtering_pb_k_kernel(tc, head_res, W_merge, g_m,
         c_raw_pool = ctx.enter_context(tc.tile_pool(name="c_raw", bufs=STEP_PASSES * (AHEAD + 1)))
         w_grouped_pool = ctx.enter_context(tc.tile_pool(name="w_grouped", bufs=4))
         c_grouped_pool = ctx.enter_context(tc.tile_pool(name="c_grouped", bufs=4))
-        w_mx_pool = ctx.enter_context(tc.tile_pool(name="w_mx", bufs=12))
-        c_mx_pool = ctx.enter_context(tc.tile_pool(name="c_mx", bufs=6))
+        w_mx_pool = ctx.enter_context(tc.tile_pool(name="w_mx", bufs=14))
+        c_mx_pool = ctx.enter_context(tc.tile_pool(name="c_mx", bufs=10))
         result_pool = ctx.enter_context(tc.tile_pool(name="result", bufs=O_TILES))
         acc_pool = ctx.enter_context(tc.psum_pool(name="acc", bufs=O_TILES))
         wt_pool = ctx.enter_context(tc.psum_pool(name="wt", bufs=4))
@@ -60,6 +61,15 @@ def tile_block_height_reducing_filtering_pb_k_kernel(tc, head_res, W_merge, g_m,
         for t in range(O_TILES):
             acc_t = acc_pool.tile([P, COLUMNS], F32, tag="acc")
             acc.append(acc_t)
+
+        def load_slab(blocks):
+            (c, t), (d, u) = blocks
+            w_raw = w_raw_pool.tile([P, len(blocks) * BLOCK_PASSES * K_PASS], BF16)
+            width = BLOCK_PASSES * K_PASS
+            w_raws[c, t], w_raws[d, u] = w_raw[:, 0:width], w_raw[:, width : 2 * width]
+            nc.sync.dma_start(
+                out=w_raw[:], in_=W_merge[t * P : (t + 1) * P, c * width : (d + 1) * width]
+            )
 
         def load_blocks(blocks, parts):
             c, t0 = blocks[0]
@@ -152,6 +162,9 @@ def tile_block_height_reducing_filtering_pb_k_kernel(tc, head_res, W_merge, g_m,
         def step_blocks(i):
             if not 0 <= i < STEPS:
                 return []
+            if i < SLAB_STEPS:
+                n, t = divmod(i, O_TILES)
+                return [(STEP_BLOCKS * n + j, t) for j in range(STEP_BLOCKS)]
             blocks = [divmod(STEP_BLOCKS * i + j, O_TILES) for j in range(STEP_BLOCKS)]
             return [block for block in blocks if block != last]
 
@@ -162,9 +175,21 @@ def tile_block_height_reducing_filtering_pb_k_kernel(tc, head_res, W_merge, g_m,
         first, second, third, fourth = range(PASSES - BLOCK_PASSES, PASSES)
         late = (CHUNKS - 1, O_TILES - 2)
 
+        def step_products(i):
+            products = []
+            for j in range(max(0, i - O_TILES), i - 1):
+                n = j // O_TILES
+                for t in range(O_TILES):
+                    slab_ready = O_TILES * n + t + 1 if j < SLAB_STEPS else 0
+                    if max(slab_ready, j + 2) == i:
+                        products += [(STEP_PASSES * j + k, t) for k in range(STEP_PASSES)]
+            return sorted(products)
+
         def load_step(i):
             if i < STEPS - 1:
-                if step_blocks(i):
+                if i < SLAB_STEPS:
+                    load_slab(step_blocks(i))
+                else:
                     load_blocks(step_blocks(i), 1)
                 for q in step_passes(i):
                     load_pass(q)
@@ -204,6 +229,7 @@ def tile_block_height_reducing_filtering_pb_k_kernel(tc, head_res, W_merge, g_m,
             load_step(i + AHEAD)
             blocks, passes = step_blocks(i), step_passes(i)
             ready_blocks, ready_passes = step_blocks(i - 1), step_passes(i - 1)
+            products = step_products(i)
             vector_groups = 22
             for block in ready_blocks:
                 quantise_block(*block, 0, BLOCK_BANKS)
@@ -216,10 +242,9 @@ def tile_block_height_reducing_filtering_pb_k_kernel(tc, head_res, W_merge, g_m,
                     quantise_pass(ready_passes[1])
                 if passes:
                     regroup_pass(passes[j], vector_groups)
-                if ready_passes:
-                    for t in range(O_TILES):
-                        if (ready_passes[j] // BLOCK_PASSES, t) != last:
-                            multiply(ready_passes[j], t)
+                half = len(products) // 2
+                for q, t in products[half:] if j else products[:half]:
+                    multiply(q, t)
             if passes:
                 quantise_pass(passes[0])
 

@@ -23,18 +23,22 @@ EPS = 1e-5
 O_TILES = OUT_CHANNELS // P
 COLUMNS = SAMPLES * POSITIONS
 PASSES = HEADS * CHANNELS // K_PASS
-BLOCK_PASSES = 4
+PART_PASSES = 4
+PART_CHANNELS = PART_PASSES * K_PASS
 BANK_PASSES = 2
-BLOCK_BANKS = BLOCK_PASSES // BANK_PASSES
+PART_BANKS = PART_PASSES // BANK_PASSES
 BANK_WORDS = BANK_PASSES * P
-CHUNKS = PASSES // BLOCK_PASSES
-STEP_BLOCKS = 2
+SLAB_PARTS = CHANNELS // PART_CHANNELS
+LAST_PART = (HEADS * SLAB_PARTS - 1, O_TILES - 1)
 STEP_PASSES = 2
-STEPS = CHUNKS * O_TILES // STEP_BLOCKS
-SLAB_STEPS = (HEADS - 1) * O_TILES
+SLAB_STEPS = HEADS * O_TILES
+LAG = 3
+LAST_STEP = SLAB_STEPS + LAG - 1
 AHEAD = 6
 RUN = 4
 GROUPS = POSITIONS // RUN
+VECTOR_GROUPS = (16, 20, 22)
+LAST_VECTOR_GROUPS = 18
 
 FLOPS = 2 * OUT_CHANNELS * HEADS * CHANNELS * COLUMNS
 
@@ -48,7 +52,7 @@ def tile_block_height_reducing_filtering_pb_k_kernel(tc, head_res, W_merge, g_m,
         w_grouped_pool = ctx.enter_context(tc.tile_pool(name="w_grouped", bufs=4))
         c_grouped_pool = ctx.enter_context(tc.tile_pool(name="c_grouped", bufs=4))
         w_mx_pool = ctx.enter_context(tc.tile_pool(name="w_mx", bufs=14))
-        c_mx_pool = ctx.enter_context(tc.tile_pool(name="c_mx", bufs=10))
+        c_mx_pool = ctx.enter_context(tc.tile_pool(name="c_mx", bufs=6))
         result_pool = ctx.enter_context(tc.tile_pool(name="result", bufs=O_TILES))
         acc_pool = ctx.enter_context(tc.psum_pool(name="acc", bufs=O_TILES))
         wt_pool = ctx.enter_context(tc.psum_pool(name="wt", bufs=4))
@@ -62,27 +66,16 @@ def tile_block_height_reducing_filtering_pb_k_kernel(tc, head_res, W_merge, g_m,
             acc_t = acc_pool.tile([P, COLUMNS], F32, tag="acc")
             acc.append(acc_t)
 
-        def load_slab(blocks):
-            (c, t), (d, u) = blocks
-            w_raw = w_raw_pool.tile([P, len(blocks) * BLOCK_PASSES * K_PASS], BF16)
-            width = BLOCK_PASSES * K_PASS
-            w_raws[c, t], w_raws[d, u] = w_raw[:, 0:width], w_raw[:, width : 2 * width]
-            nc.sync.dma_start(
-                out=w_raw[:], in_=W_merge[t * P : (t + 1) * P, c * width : (d + 1) * width]
-            )
-
-        def load_blocks(blocks, parts):
-            c, t0 = blocks[0]
-            w_raw = w_raw_pool.tile([P, STEP_BLOCKS, BLOCK_PASSES * K_PASS], BF16)
-            for j in range(len(blocks)):
-                w_raws[c, t0 + j] = w_raw[:, j]
-            width = BLOCK_PASSES * K_PASS // parts
-            for h in range(parts):
-                k0 = c * BLOCK_PASSES * K_PASS + h * width
-                rows = W_merge[t0 * P : (t0 + len(blocks)) * P, k0 : k0 + width]
+        def load_parts(parts, pieces):
+            c0, t = parts[0]
+            w_raw = w_raw_pool.tile([P, SLAB_PARTS * PART_CHANNELS], BF16)
+            for j in range(len(parts)):
+                w_raws[parts[j]] = w_raw[:, j * PART_CHANNELS : (j + 1) * PART_CHANNELS]
+            width = len(parts) * PART_CHANNELS // pieces
+            for h in range(pieces):
+                k0 = c0 * PART_CHANNELS + h * width
                 nc.sync.dma_start(
-                    out=w_raw[:, 0 : len(blocks), h * width : (h + 1) * width],
-                    in_=rows.rearrange("(t o) k -> o t k", o=P),
+                    out=w_raw[:, h * width : (h + 1) * width], in_=W_merge[t * P : (t + 1) * P, k0 : k0 + width]
                 )
 
         def load_pass(q):
@@ -100,20 +93,20 @@ def tile_block_height_reducing_filtering_pb_k_kernel(tc, head_res, W_merge, g_m,
                     nc.tensor.transpose(wt[:, i, s, :], words[:, h * BANK_PASSES + i, s, :], ident[:])
             return wt
 
-        def empty_bank(copy, c, t, h, wt):
+        def empty_bank(c, t, h, wt):
             if h == 0:
-                w_grouped = w_grouped_pool.tile([P, BLOCK_PASSES, P, PACK], BF16, align_bytes=64)
+                w_grouped = w_grouped_pool.tile([P, PART_PASSES, P, PACK], BF16, align_bytes=64)
                 w_groupeds[c, t] = w_grouped
             words = w_groupeds[c, t][:].bitcast(F32)
-            copy(
+            nc.scalar.copy(
                 out=words[:, h * BANK_PASSES : (h + 1) * BANK_PASSES],
                 in_=wt[:].rearrange("p g s o -> p g o s"),
             )
 
-        def quantise_block(c, t, h0, h1):
+        def quantise_part(c, t, h0, h1):
             if h0 == 0:
-                w_code = w_mx_pool.tile([P, BLOCK_BANKS * BANK_WORDS], U32, align_bytes=64)
-                w_scale = w_mx_pool.tile([P, BLOCK_BANKS * BANK_WORDS], U8, align_bytes=64)
+                w_code = w_mx_pool.tile([P, PART_BANKS * BANK_WORDS], U32, align_bytes=64)
+                w_scale = w_mx_pool.tile([P, PART_BANKS * BANK_WORDS], U8, align_bytes=64)
                 w_codes[c, t], w_scales[c, t] = w_code, w_scale
             cols = slice(h0 * BANK_WORDS, h1 * BANK_WORDS)
             nc.vector.quantize_mx(
@@ -122,15 +115,11 @@ def tile_block_height_reducing_filtering_pb_k_kernel(tc, head_res, W_merge, g_m,
                 in_=w_groupeds[c, t][:, h0 * BANK_PASSES : h1 * BANK_PASSES].rearrange("p g o t -> p (g o t)"),
             )
 
-        def regroup_views(q):
-            src = c_raws[q][:].rearrange("p b (t c i) -> p b c t i", t=PACK, i=RUN)
-            dst = c_groupeds[q][:].rearrange("p (b c i) t -> p b c t i", b=SAMPLES, i=RUN)
-            return dst, src
-
         def regroup_pass(q, vector_groups):
             c_grouped = c_grouped_pool.tile([P, COLUMNS, PACK], BF16, align_bytes=64)
             c_groupeds[q] = c_grouped
-            dst, src = regroup_views(q)
+            src = c_raws[q][:].rearrange("p b (t c i) -> p b c t i", t=PACK, i=RUN)
+            dst = c_grouped[:].rearrange("p (b c i) t -> p b c t i", b=SAMPLES, i=RUN)
             nc.vector.tensor_copy(out=dst[:, :, 0:vector_groups], in_=src[:, :, 0:vector_groups])
             nc.scalar.copy(out=dst[:, :, vector_groups:GROUPS], in_=src[:, :, vector_groups:GROUPS])
 
@@ -145,7 +134,7 @@ def tile_block_height_reducing_filtering_pb_k_kernel(tc, head_res, W_merge, g_m,
             )
 
         def multiply(q, t):
-            c, g = divmod(q, BLOCK_PASSES)
+            c, g = divmod(q, PART_PASSES)
             cols = slice(g * P, (g + 1) * P)
             nc.tensor.matmul_mx(
                 out=acc[t][:],
@@ -157,56 +146,36 @@ def tile_block_height_reducing_filtering_pb_k_kernel(tc, head_res, W_merge, g_m,
                 stop=(q == PASSES - 1),
             )
 
-        last = (CHUNKS - 1, O_TILES - 1)
+        def multiply_pass(q):
+            for t in range(O_TILES):
+                if (q // PART_PASSES, t) != LAST_PART:
+                    multiply(q, t)
 
-        def step_blocks(i):
-            if not 0 <= i < STEPS:
+        def step_parts(i):
+            if not 0 <= i < SLAB_STEPS:
                 return []
-            if i < SLAB_STEPS:
-                n, t = divmod(i, O_TILES)
-                return [(STEP_BLOCKS * n + j, t) for j in range(STEP_BLOCKS)]
-            blocks = [divmod(STEP_BLOCKS * i + j, O_TILES) for j in range(STEP_BLOCKS)]
-            return [block for block in blocks if block != last]
+            n, t = divmod(i, O_TILES)
+            parts = [(SLAB_PARTS * n + j, t) for j in range(SLAB_PARTS)]
+            return [part for part in parts if part != LAST_PART]
 
         def step_passes(i):
-            q = STEP_PASSES * (i - 1)
+            q = STEP_PASSES * (i - LAG)
             return [q, q + 1] if 0 <= q < PASSES else []
 
-        first, second, third, fourth = range(PASSES - BLOCK_PASSES, PASSES)
-        late = (CHUNKS - 1, O_TILES - 2)
-
-        def step_products(i):
-            products = []
-            for j in range(max(0, i - O_TILES), i - 1):
-                n = j // O_TILES
-                for t in range(O_TILES):
-                    slab_ready = O_TILES * n + t + 1 if j < SLAB_STEPS else 0
-                    if max(slab_ready, j + 2) == i:
-                        products += [(STEP_PASSES * j + k, t) for k in range(STEP_PASSES)]
-            return sorted(products)
-
         def load_step(i):
-            if i < STEPS - 1:
-                if i < SLAB_STEPS:
-                    load_slab(step_blocks(i))
-                else:
-                    load_blocks(step_blocks(i), 1)
-                for q in step_passes(i):
-                    load_pass(q)
-            elif i == STEPS - 1:
-                load_blocks([late], 1)
-                load_pass(first)
-                load_pass(second)
-            elif i == STEPS:
-                load_pass(third)
-                load_pass(fourth)
-                load_blocks([last], BLOCK_BANKS)
+            parts = step_parts(i)
+            if parts:
+                load_parts(parts, 1)
+            for q in step_passes(i):
+                load_pass(q)
+            if i == LAST_STEP:
+                load_parts([LAST_PART], PART_BANKS)
 
         gb_rows = const.tile([P, P], BF16)
         nc.vector.memset(gb_rows[:], 0.0)
         nc.scalar.dma_start(out=gb_rows[0:O_TILES, :], in_=g_m.rearrange("(t o) -> t o", o=P))
         nc.scalar.dma_start(out=gb_rows[O_TILES : 2 * O_TILES, :], in_=b_m.rearrange("(t o) -> t o", o=P))
-        for i in range(2):
+        for i in range(AHEAD):
             load_step(i)
         ident = const.tile([P, P], F32)
         make_identity(nc, ident[:])
@@ -216,76 +185,56 @@ def tile_block_height_reducing_filtering_pb_k_kernel(tc, head_res, W_merge, g_m,
         nc.vector.memset(eps[:], EPS)
         first_root = const.tile([P, 1], F32)
         nc.scalar.activation(out=first_root[:], in_=eps[:], func=ACT.Abs_reciprocal_sqrt)
-        for i in range(2, AHEAD):
-            load_step(i)
 
-        for i in range(STEPS - 1):
-            if i == 3:
+        for i in range(LAST_STEP):
+            load_step(i + AHEAD)
+            if i == LAG:
                 gb_bank = wt_pool.tile([P, P], BF16, tag="wt")
                 nc.tensor.transpose(gb_bank[:], gb_rows[:], ident_bf16[:])
                 gb = const.tile([P, 2 * O_TILES], F32)
                 nc.scalar.copy(out=gb[:], in_=gb_bank[:, 0 : 2 * O_TILES])
                 g_cols, b_cols = gb[:, 0:O_TILES], gb[:, O_TILES : 2 * O_TILES]
-            load_step(i + AHEAD)
-            blocks, passes = step_blocks(i), step_passes(i)
-            ready_blocks, ready_passes = step_blocks(i - 1), step_passes(i - 1)
-            products = step_products(i)
-            vector_groups = 22
-            for block in ready_blocks:
-                quantise_block(*block, 0, BLOCK_BANKS)
-            for j in range(STEP_BLOCKS):
-                if j < len(blocks):
-                    banks = [transpose_bank(*blocks[j], h) for h in range(BLOCK_BANKS)]
-                    for h in range(BLOCK_BANKS):
-                        empty_bank(nc.scalar.copy, *blocks[j], h, banks[h])
+            parts, passes = step_parts(i), step_passes(i)
+            ready_parts, ready_passes = step_parts(i - 1), step_passes(i - 1)
+            for part in ready_parts:
+                quantise_part(*part, 0, PART_BANKS)
+            for j in range(STEP_PASSES):
+                if j < len(parts):
+                    banks = [transpose_bank(*parts[j], h) for h in range(PART_BANKS)]
+                    for h in range(PART_BANKS):
+                        empty_bank(*parts[j], h, banks[h])
                 if j == 1 and ready_passes:
                     quantise_pass(ready_passes[1])
                 if passes:
-                    regroup_pass(passes[j], vector_groups)
-                half = len(products) // 2
-                for q, t in products[half:] if j else products[:half]:
-                    multiply(q, t)
+                    regroup_pass(passes[j], VECTOR_GROUPS[len(parts)])
+                if ready_passes:
+                    multiply_pass(ready_passes[j])
             if passes:
                 quantise_pass(passes[0])
 
-        def multiply_early_tiles(q):
-            for t in range(O_TILES - 1):
-                multiply(q, t)
-
-        for block in step_blocks(STEPS - 2):
-            quantise_block(*block, 0, BLOCK_BANKS)
-        banks = [transpose_bank(*late, h) for h in range(BLOCK_BANKS)]
-        regroup_pass(first, 20)
-        for t in range(O_TILES):
-            multiply(first - 2, t)
-        for h in range(BLOCK_BANKS):
-            empty_bank(nc.scalar.copy, *late, h, banks[h])
-        quantise_pass(first - 1)
-        regroup_pass(second, 20)
-        quantise_pass(first)
-        for t in range(O_TILES):
-            multiply(first - 1, t)
-        quantise_block(*late, 0, BLOCK_BANKS)
+        first, second, third, fourth = range(PASSES - PART_PASSES, PASSES)
         quantise_pass(second)
-        regroup_pass(third, 18)
-        multiply_early_tiles(first)
-        multiply_early_tiles(second)
-        banks = [transpose_bank(*last, h) for h in range(BLOCK_BANKS)]
-        regroup_pass(fourth, 18)
+        regroup_pass(third, LAST_VECTOR_GROUPS)
+        multiply_pass(first)
+        multiply_pass(second)
+        banks = [transpose_bank(*LAST_PART, h) for h in range(PART_BANKS)]
+        regroup_pass(fourth, LAST_VECTOR_GROUPS)
         quantise_pass(third)
+        for h in range(PART_BANKS):
+            empty_bank(*LAST_PART, h, banks[h])
         quantise_pass(fourth)
-        for h in range(BLOCK_BANKS):
-            empty_bank(nc.scalar.copy, *last, h, banks[h])
         for t in range(O_TILES - 1):
             multiply(third, t)
             multiply(fourth, t)
+
         stats = const.tile([P, O_TILES, 6], F32)
         mean_var = const.tile([P, O_TILES, 2], F32)
         inv_std = const.tile([P, O_TILES], F32)
-        gain = const.tile([P, O_TILES], F32)
         early_gain = const.tile([P, 2], F32)
+        early_mean_gain = const.tile([P, 2], F32)
         early_shift = const.tile([P, 2], F32)
-        minus_mean_g = const.tile([P, 1], F32)
+        gain = const.tile([P, O_TILES], F32)
+        minus_mean_g = const.tile([P, O_TILES], F32)
         shift = const.tile([P, O_TILES], F32)
         results = []
         for t in range(O_TILES):
@@ -307,12 +256,15 @@ def tile_block_height_reducing_filtering_pb_k_kernel(tc, head_res, W_merge, g_m,
                 scale=1.0,
             )
 
-        def find_gain(t):
-            nc.vector.tensor_mul(out=gain[:, t : t + 1], in0=g_cols[:, t : t + 1], in1=inv_std[:, t : t + 1])
+        def find_early_gain_shift(t):
+            col = slice(t, t + 1)
+            nc.gpsimd.tensor_mul(out=early_gain[:, col], in0=g_cols[:, col], in1=inv_std[:, col])
+            nc.gpsimd.tensor_mul(out=early_mean_gain[:, col], in0=mean_var[:, t, 0:1], in1=early_gain[:, col])
+            nc.gpsimd.tensor_sub(out=early_shift[:, col], in0=b_cols[:, col], in1=early_mean_gain[:, col])
 
         def find_minus_mean_g(t):
             nc.vector.scalar_tensor_tensor(
-                out=minus_mean_g[:],
+                out=minus_mean_g[:, t : t + 1],
                 in0=mean_var[:, t, 0:1],
                 scalar=-1.0,
                 in1=g_cols[:, t : t + 1],
@@ -320,29 +272,22 @@ def tile_block_height_reducing_filtering_pb_k_kernel(tc, head_res, W_merge, g_m,
                 op1=ALU.mult,
             )
 
+        def find_gain(t):
+            nc.vector.tensor_mul(out=gain[:, t : t + 1], in0=g_cols[:, t : t + 1], in1=inv_std[:, t : t + 1])
+
         def find_shift(t):
             nc.vector.scalar_tensor_tensor(
                 out=shift[:, t : t + 1],
-                in0=minus_mean_g[:],
+                in0=minus_mean_g[:, t : t + 1],
                 scalar=inv_std[:, t : t + 1],
                 in1=b_cols[:, t : t + 1],
                 op0=ALU.mult,
                 op1=ALU.add,
             )
 
-        def find_gain_shift_on_gpsimd(t):
-            mean_gain = const.tile([P, 1], F32, name="mean_gain")
-            nc.gpsimd.tensor_mul(out=early_gain[:, t : t + 1], in0=g_cols[:, t : t + 1], in1=inv_std[:, t : t + 1])
-            nc.gpsimd.tensor_mul(out=mean_gain[:], in0=mean_var[:, t, 0:1], in1=early_gain[:, t : t + 1])
-            nc.gpsimd.tensor_sub(out=early_shift[:, t : t + 1], in0=b_cols[:, t : t + 1], in1=mean_gain[:])
-
-        def scalar_relu(t):
+        def scalar_relu(t, gains, shifts):
             nc.scalar.activation(
-                out=results[t][:],
-                in_=acc[t][:],
-                func=ACT.Relu,
-                bias=(early_shift if t < 2 else shift)[:, t : t + 1],
-                scale=(early_gain if t < 2 else gain)[:, t : t + 1],
+                out=results[t][:], in_=acc[t][:], func=ACT.Relu, bias=shifts[:, t : t + 1], scale=gains[:, t : t + 1]
             )
 
         def vector_relu(t):
@@ -364,25 +309,25 @@ def tile_block_height_reducing_filtering_pb_k_kernel(tc, head_res, W_merge, g_m,
                 in_=results[t][:].rearrange("o (b d) -> o b d", b=SAMPLES),
             )
 
-        quantise_block(*last, 0, 1)
-        quantise_block(*last, 1, 2)
+        quantise_part(*LAST_PART, 0, 1)
         find_stats(0)
+        quantise_part(*LAST_PART, 1, 2)
         for q in (first, second, third, fourth):
             multiply(q, O_TILES - 1)
         find_mean_var(0)
         find_inv_std(0)
-        find_gain_shift_on_gpsimd(0)
+        find_early_gain_shift(0)
         find_stats(1)
         find_mean_var(1)
         find_inv_std(1)
-        scalar_relu(0)
+        scalar_relu(0, early_gain, early_shift)
         store(0)
-        find_gain_shift_on_gpsimd(1)
+        find_early_gain_shift(1)
         find_stats(2)
         find_stats(3)
         find_mean_var(2)
         find_mean_var(3)
-        scalar_relu(1)
+        scalar_relu(1, early_gain, early_shift)
         store(1)
         find_inv_std(2)
         find_inv_std(3)
@@ -390,7 +335,7 @@ def tile_block_height_reducing_filtering_pb_k_kernel(tc, head_res, W_merge, g_m,
         find_gain(2)
         find_gain(3)
         find_shift(3)
-        scalar_relu(3)
+        scalar_relu(3, gain, shift)
         store(3)
         vector_relu(2)
         store(2)

from contextlib import ExitStack

import concourse.mybir as mybir
from concourse.masks import make_identity

F32 = mybir.dt.float32
BF16 = mybir.dt.bfloat16
U32 = mybir.dt.uint32
U8 = mybir.dt.uint8
FP8X4 = mybir.dt.float8_e4m3fn_x4
ACT = mybir.ActivationFunctionType
ALU = mybir.AluOpType

P = 128
PACK = 4
K_PASS = P * PACK
PAIR = 2

HEADS, SAMPLES, CHANNELS, POSITIONS = 4, 4, 4096, 128
OUT_CHANNELS = 512
EPS = 1e-5

O_TILES = OUT_CHANNELS // P
COLUMNS = SAMPLES * POSITIONS
PASSES = HEADS * CHANNELS // K_PASS
PART_PASSES = 4
PART_CHANNELS = PART_PASSES * K_PASS
BANK_PASSES = 2
PART_BANKS = PART_PASSES // BANK_PASSES
BANK_WORDS = BANK_PASSES * P
SLAB_PARTS = CHANNELS // PART_CHANNELS
LAST_PART = (HEADS * SLAB_PARTS - 1, O_TILES - 1)
STEP_PASSES = 2
SLAB_STEPS = HEADS * O_TILES
LAG = 3
LAST_STEP = SLAB_STEPS + LAG - 1
AHEAD = 6
RUN = 4
GROUPS = POSITIONS // RUN
VECTOR_GROUPS = (16, 20, 22)
LAST_VECTOR_GROUPS = 18

FLOPS = 2 * OUT_CHANNELS * HEADS * CHANNELS * COLUMNS


def tile_block_height_reducing_filtering_pb_k_kernel(tc, head_res, W_merge, g_m, b_m, out):
    nc = tc.nc
    with ExitStack() as ctx:
        const = ctx.enter_context(tc.tile_pool(name="const", bufs=1))
        w_raw_pool = ctx.enter_context(tc.tile_pool(name="w_raw", bufs=AHEAD + 1))
        c_raw_pool = ctx.enter_context(tc.tile_pool(name="c_raw", bufs=STEP_PASSES * (AHEAD + 1)))
        w_grouped_pool = ctx.enter_context(tc.tile_pool(name="w_grouped", bufs=4))
        c_grouped_pool = ctx.enter_context(tc.tile_pool(name="c_grouped", bufs=4))
        w_mx_pool = ctx.enter_context(tc.tile_pool(name="w_mx", bufs=14))
        c_mx_pool = ctx.enter_context(tc.tile_pool(name="c_mx", bufs=6))
        result_pool = ctx.enter_context(tc.tile_pool(name="result", bufs=O_TILES))
        acc_pool = ctx.enter_context(tc.psum_pool(name="acc", bufs=O_TILES))
        wt_pool = ctx.enter_context(tc.psum_pool(name="wt", bufs=4))
        ctx.enter_context(tc.manual_schedule())

        w_raws, w_groupeds, w_codes, w_scales = {}, {}, {}, {}
        c_raws, c_groupeds, c_codes, c_scales = {}, {}, {}, {}

        acc = []
        for t in range(O_TILES):
            acc_t = acc_pool.tile([P, COLUMNS], F32, tag="acc")
            acc.append(acc_t)

        def load_parts(parts, pieces):
            c0, t = parts[0]
            w_raw = w_raw_pool.tile([P, SLAB_PARTS * PART_CHANNELS], BF16)
            for j in range(len(parts)):
                w_raws[parts[j]] = w_raw[:, j * PART_CHANNELS : (j + 1) * PART_CHANNELS]
            width = len(parts) * PART_CHANNELS // pieces
            for h in range(pieces):
                k0 = c0 * PART_CHANNELS + h * width
                nc.sync.dma_start(
                    out=w_raw[:, h * width : (h + 1) * width], in_=W_merge[t * P : (t + 1) * P, k0 : k0 + width]
                )

        def load_pass(q):
            n, g = divmod(q, CHANNELS // K_PASS)
            c_raw = c_raw_pool.tile([P, SAMPLES, PACK * POSITIONS], BF16)
            rows = head_res[n, :, g * K_PASS : (g + 1) * K_PASS, :]
            nc.sync.dma_start(out=c_raw[:], in_=rows.rearrange("b (p j) w -> p b (j w)", j=PACK))
            c_raws[q] = c_raw

        def transpose_bank(c, t, h):
            words = w_raws[c, t].bitcast(F32).rearrange("o (g p s) -> o g s p", p=P, s=PAIR)
            wt = wt_pool.tile([P, BANK_PASSES, PAIR, P], F32)
            for i in range(BANK_PASSES):
                for s in range(PAIR):
                    nc.tensor.transpose(wt[:, i, s, :], words[:, h * BANK_PASSES + i, s, :], ident[:])
            return wt

        def empty_bank(c, t, h, wt):
            if h == 0:
                w_grouped = w_grouped_pool.tile([P, PART_PASSES, P, PACK], BF16, align_bytes=64)
                w_groupeds[c, t] = w_grouped
            words = w_groupeds[c, t][:].bitcast(F32)
            nc.scalar.copy(
                out=words[:, h * BANK_PASSES : (h + 1) * BANK_PASSES],
                in_=wt[:].rearrange("p g s o -> p g o s"),
            )

        def quantise_part(c, t, h0, h1):
            if h0 == 0:
                w_code = w_mx_pool.tile([P, PART_BANKS * BANK_WORDS], U32, align_bytes=64)
                w_scale = w_mx_pool.tile([P, PART_BANKS * BANK_WORDS], U8, align_bytes=64)
                w_codes[c, t], w_scales[c, t] = w_code, w_scale
            cols = slice(h0 * BANK_WORDS, h1 * BANK_WORDS)
            nc.vector.quantize_mx(
                out=w_codes[c, t][:, cols].bitcast(FP8X4),
                scales=w_scales[c, t][:, cols],
                in_=w_groupeds[c, t][:, h0 * BANK_PASSES : h1 * BANK_PASSES].rearrange("p g o t -> p (g o t)"),
            )

        def regroup_pass(q, vector_groups):
            c_grouped = c_grouped_pool.tile([P, COLUMNS, PACK], BF16, align_bytes=64)
            c_groupeds[q] = c_grouped
            src = c_raws[q][:].rearrange("p b (t c i) -> p b c t i", t=PACK, i=RUN)
            dst = c_grouped[:].rearrange("p (b c i) t -> p b c t i", b=SAMPLES, i=RUN)
            nc.vector.tensor_copy(out=dst[:, :, 0:vector_groups], in_=src[:, :, 0:vector_groups])
            nc.scalar.copy(out=dst[:, :, vector_groups:GROUPS], in_=src[:, :, vector_groups:GROUPS])

        def quantise_pass(q):
            c_code = c_mx_pool.tile([P, COLUMNS], U32, align_bytes=64)
            c_scale = c_mx_pool.tile([P, COLUMNS], U8, align_bytes=64)
            c_codes[q], c_scales[q] = c_code, c_scale
            nc.vector.quantize_mx(
                out=c_code[:].bitcast(FP8X4),
                scales=c_scale[:],
                in_=c_groupeds[q][:].rearrange("p c t -> p (c t)"),
            )

        def multiply(q, t):
            c, g = divmod(q, PART_PASSES)
            cols = slice(g * P, (g + 1) * P)
            nc.tensor.matmul_mx(
                out=acc[t][:],
                lhsT=w_codes[c, t][:, cols].bitcast(FP8X4),
                lhsT_scale=w_scales[c, t][:, cols],
                rhs=c_codes[q][:].bitcast(FP8X4),
                rhs_scale=c_scales[q][:],
                start=(q == 0),
                stop=(q == PASSES - 1),
            )

        def multiply_pass(q):
            for t in range(O_TILES):
                if (q // PART_PASSES, t) != LAST_PART:
                    multiply(q, t)

        def step_parts(i):
            if not 0 <= i < SLAB_STEPS:
                return []
            n, t = divmod(i, O_TILES)
            parts = [(SLAB_PARTS * n + j, t) for j in range(SLAB_PARTS)]
            return [part for part in parts if part != LAST_PART]

        def step_passes(i):
            q = STEP_PASSES * (i - LAG)
            return [q, q + 1] if 0 <= q < PASSES else []

        def load_step(i):
            parts = step_parts(i)
            if parts:
                load_parts(parts, 1)
            for q in step_passes(i):
                load_pass(q)
            if i == LAST_STEP:
                load_parts([LAST_PART], PART_BANKS)

        gb_rows = const.tile([P, P], BF16)
        nc.vector.memset(gb_rows[:], 0.0)
        nc.scalar.dma_start(out=gb_rows[0:O_TILES, :], in_=g_m.rearrange("(t o) -> t o", o=P))
        nc.scalar.dma_start(out=gb_rows[O_TILES : 2 * O_TILES, :], in_=b_m.rearrange("(t o) -> t o", o=P))
        for i in range(AHEAD):
            load_step(i)
        ident = const.tile([P, P], F32)
        make_identity(nc, ident[:])
        ident_bf16 = const.tile([P, P], BF16)
        make_identity(nc, ident_bf16[:])
        eps = const.tile([P, 1], F32)
        nc.vector.memset(eps[:], EPS)
        first_root = const.tile([P, 1], F32)
        nc.scalar.activation(out=first_root[:], in_=eps[:], func=ACT.Abs_reciprocal_sqrt)

        for i in range(LAST_STEP):
            load_step(i + AHEAD)
            if i == LAG:
                gb_bank = wt_pool.tile([P, P], BF16, tag="wt")
                nc.tensor.transpose(gb_bank[:], gb_rows[:], ident_bf16[:])
                gb = const.tile([P, 2 * O_TILES], F32)
                nc.scalar.copy(out=gb[:], in_=gb_bank[:, 0 : 2 * O_TILES])
                g_cols, b_cols = gb[:, 0:O_TILES], gb[:, O_TILES : 2 * O_TILES]
            parts, passes = step_parts(i), step_passes(i)
            ready_parts, ready_passes = step_parts(i - 1), step_passes(i - 1)
            for part in ready_parts:
                quantise_part(*part, 0, PART_BANKS)
            for j in range(STEP_PASSES):
                if j < len(parts):
                    banks = [transpose_bank(*parts[j], h) for h in range(PART_BANKS)]
                    for h in range(PART_BANKS):
                        empty_bank(*parts[j], h, banks[h])
                if j == 1 and ready_passes:
                    quantise_pass(ready_passes[1])
                if passes:
                    regroup_pass(passes[j], VECTOR_GROUPS[len(parts)])
                if ready_passes:
                    multiply_pass(ready_passes[j])
            if passes:
                quantise_pass(passes[0])

        first, second, third, fourth = range(PASSES - PART_PASSES, PASSES)
        quantise_pass(second)
        regroup_pass(third, LAST_VECTOR_GROUPS)
        multiply_pass(first)
        multiply_pass(second)
        banks = [transpose_bank(*LAST_PART, h) for h in range(PART_BANKS)]
        regroup_pass(fourth, LAST_VECTOR_GROUPS)
        quantise_pass(third)
        for h in range(PART_BANKS):
            empty_bank(*LAST_PART, h, banks[h])
        quantise_pass(fourth)
        for t in range(O_TILES - 1):
            multiply(third, t)
            multiply(fourth, t)

        stats = const.tile([P, O_TILES, 6], F32)
        mean_var = const.tile([P, O_TILES, 2], F32)
        inv_std = const.tile([P, O_TILES], F32)
        early_gain = const.tile([P, 2], F32)
        early_mean_gain = const.tile([P, 2], F32)
        early_shift = const.tile([P, 2], F32)
        gain = const.tile([P, O_TILES], F32)
        minus_mean_g = const.tile([P, O_TILES], F32)
        shift = const.tile([P, O_TILES], F32)
        results = []
        for t in range(O_TILES):
            result = result_pool.tile([P, COLUMNS], F32)
            results.append(result)

        def find_stats(t):
            nc.vector.bn_stats(out=stats[:, t, :], in_=acc[t][:])

        def find_mean_var(t):
            nc.vector.bn_aggr(out=mean_var[:, t, :], in_=stats[:, t, :])

        def find_inv_std(t):
            nc.scalar.activation(
                out=inv_std[:, t : t + 1],
                in_=mean_var[:, t, 1:2],
                func=ACT.Abs_reciprocal_sqrt,
                bias=eps[:, 0:1],
                scale=1.0,
            )

        def find_early_gain_shift(t):
            col = slice(t, t + 1)
            nc.gpsimd.tensor_mul(out=early_gain[:, col], in0=g_cols[:, col], in1=inv_std[:, col])
            nc.gpsimd.tensor_mul(out=early_mean_gain[:, col], in0=mean_var[:, t, 0:1], in1=early_gain[:, col])
            nc.gpsimd.tensor_sub(out=early_shift[:, col], in0=b_cols[:, col], in1=early_mean_gain[:, col])

        def find_minus_mean_g(t):
            nc.vector.scalar_tensor_tensor(
                out=minus_mean_g[:, t : t + 1],
                in0=mean_var[:, t, 0:1],
                scalar=-1.0,
                in1=g_cols[:, t : t + 1],
                op0=ALU.mult,
                op1=ALU.mult,
            )

        def find_gain(t):
            nc.vector.tensor_mul(out=gain[:, t : t + 1], in0=g_cols[:, t : t + 1], in1=inv_std[:, t : t + 1])

        def find_shift(t):
            nc.vector.scalar_tensor_tensor(
                out=shift[:, t : t + 1],
                in0=minus_mean_g[:, t : t + 1],
                scalar=inv_std[:, t : t + 1],
                in1=b_cols[:, t : t + 1],
                op0=ALU.mult,
                op1=ALU.add,
            )

        def scalar_relu(t, gains, shifts):
            nc.scalar.activation(
                out=results[t][:], in_=acc[t][:], func=ACT.Relu, bias=shifts[:, t : t + 1], scale=gains[:, t : t + 1]
            )

        def vector_relu(t):
            nc.vector.tensor_scalar(
                out=results[t][:],
                in0=acc[t][:],
                scalar1=mean_var[:, t, 0:1],
                scalar2=gain[:, t : t + 1],
                op0=ALU.subtract,
                op1=ALU.mult,
            )
            nc.vector.tensor_scalar(
                out=results[t][:], in0=results[t][:], scalar1=b_cols[:, t : t + 1], scalar2=0.0, op0=ALU.add, op1=ALU.max
            )

        def store(t):
            nc.sync.dma_start(
                out=out[:, t * P : (t + 1) * P, :].rearrange("b o d -> o b d"),
                in_=results[t][:].rearrange("o (b d) -> o b d", b=SAMPLES),
            )

        quantise_part(*LAST_PART, 0, 1)
        find_stats(0)
        quantise_part(*LAST_PART, 1, 2)
        for q in (first, second, third, fourth):
            multiply(q, O_TILES - 1)
        find_mean_var(0)
        find_inv_std(0)
        find_early_gain_shift(0)
        find_stats(1)
        find_mean_var(1)
        find_inv_std(1)
        scalar_relu(0, early_gain, early_shift)
        store(0)
        find_early_gain_shift(1)
        find_stats(2)
        find_stats(3)
        find_mean_var(2)
        find_mean_var(3)
        scalar_relu(1, early_gain, early_shift)
        store(1)
        find_inv_std(2)
        find_inv_std(3)
        find_minus_mean_g(3)
        find_gain(2)
        find_gain(3)
        find_shift(3)
        scalar_relu(3, gain, shift)
        store(3)
        vector_relu(2)
        store(2)
